import numpy as np
import ml_dtypes


def mxq(x, axis, fmt="e4m3"):
    dtype, down = {"e4m3": (ml_dtypes.float8_e4m3fn, 7), "e5m2": (ml_dtypes.float8_e5m2, 14)}[fmt]
    v = np.moveaxis(np.asarray(x, np.float32).astype(ml_dtypes.bfloat16).astype(np.float64), axis, -1)
    blocks = v.reshape(v.shape[:-1] + (-1, 32))
    amax = np.abs(blocks).max(-1, keepdims=True)
    byte = np.maximum(np.where(amax > 0, np.frexp(amax)[1] - 1 + 127, 0) - down, 1)
    scale = np.exp2(byte - 127.0)
    codes = (blocks / scale).astype(np.float32).astype(dtype).astype(np.float64)
    return np.moveaxis((codes * scale).reshape(v.shape), -1, axis)


WIDE = False


def mx_kscale(k):
    if not WIDE:
        return np.ones(k)
    levels = np.array([10, -10, 5, -5, 0])
    a = np.random.permutation(np.resize(levels, k // 512 * 4)).reshape(k // 512, 4)
    idx = np.arange(k)
    return np.exp2(a[idx // 512, idx % 128 // 32])


BF16 = ml_dtypes.bfloat16


def bf(x):
    return np.asarray(x, np.float32).astype(BF16)


def f64(x):
    return np.asarray(x).astype(np.float64)


B, D, L, H = 256, 512, 128, 16384


def sigmoid(v):
    return 1.0 / (1.0 + np.exp(-v))


def setup_inputs():
    t = mx_kscale(H)
    return {
        "z": bf(np.random.standard_normal((B, L)) * 1.7),
        "x": bf(np.random.random((B, D)) < 0.5),
        "Wd1": bf(np.random.standard_normal((L, H)) * 0.6 / np.sqrt(L) * t),
        "bd1": bf(np.random.standard_normal(H) * 0.5 * t),
        "Wd2": bf(np.random.standard_normal((H, D)) * 2.8 / np.sqrt(H) / t[:, None]),
        "bd2": bf(np.random.standard_normal(D) * 0.5),
    }


def reference(z, x, Wd1, bd1, Wd2, bd2):
    x = f64(x)
    hd = np.maximum(f64(z) @ f64(Wd1) + f64(bd1), 0.0)
    theta = sigmoid((mxq(hd, 1, "e4m3") @ mxq(f64(Wd2), 0, "e4m3")) + f64(bd2))
    return np.sum(x * np.log(theta) + (1.0 - x) * np.log1p(-theta), axis=-1)

@@ -1,0 +1,238 @@
+from contextlib import ExitStack
+
+import concourse.mybir as mybir
+from concourse.masks import make_identity
+
+BF16 = mybir.dt.bfloat16
+F32 = mybir.dt.float32
+U8 = mybir.dt.uint8
+U32 = mybir.dt.uint32
+FP8X4 = mybir.dt.float8_e4m3fn_x4
+ACT = mybir.ActivationFunctionType
+ALU = mybir.AluOpType
+
+P = 128
+PACK = 4
+K_PASS = P * PACK
+
+B, D, L, H = 256, 512, 128, 16384
+PASSES = H // K_PASS
+B_TILES = B // P
+
+CHUNK_PASSES = 2
+CHUNKS = PASSES // CHUNK_PASSES
+RING = 8
+
+W2_COLS_SCALAR = 208
+W2_COLS_VECTOR = D - W2_COLS_SCALAR
+
+FLOPS = 2 * B * L * H + 2 * B * H * D
+
+
+def regroup(copy, grouped, rows):
+    copy(
+        out=grouped.rearrange("p (c i) t -> p c t i", i=4),
+        in_=rows.rearrange("p t (c i) -> p c t i", i=4),
+    )
+
+
+def tile_vae_pb_k_kernel(tc, z, x, Wd1, bd1, Wd2, bd2, out):
+    nc = tc.nc
+    with ExitStack() as ctx:
+        const = ctx.enter_context(tc.tile_pool(name="const", bufs=1))
+        weights = ctx.enter_context(tc.tile_pool(name="weights", bufs=RING))
+        stage = ctx.enter_context(tc.tile_pool(name="stage", bufs=3))
+        packed = ctx.enter_context(tc.tile_pool(name="packed", bufs=3))
+        tail = ctx.enter_context(tc.tile_pool(name="tail", bufs=2))
+        psum_acc = ctx.enter_context(tc.psum_pool(name="psum_acc", bufs=1))
+        psum = ctx.enter_context(tc.psum_pool(name="psum", bufs=6))
+
+        z_sb = const.tile([P, B_TILES, L], BF16)
+        nc.sync.dma_start(out=z_sb[:], in_=z.rearrange("(m p) l -> p m l", p=P))
+        bd1_rows = const.tile([P, K_PASS], BF16)
+        nc.vector.memset(bd1_rows[:], 0.0)
+        nc.sync.dma_start(out=bd1_rows[0:PASSES, :], in_=bd1.rearrange("(g k) -> g k", k=K_PASS))
+
+        w1_chunks = {}
+        w2_chunks = {}
+
+        def load_chunk(c):
+            units = slice(c * CHUNK_PASSES * K_PASS, (c + 1) * CHUNK_PASSES * K_PASS)
+            w1_chunks[c] = weights.tile([P, CHUNK_PASSES, K_PASS], BF16, name="w1_chunk")
+            nc.sync.dma_start(
+                out=w1_chunks[c][:], in_=Wd1[:, units].rearrange("l (s k) -> l s k", k=K_PASS)
+            )
+            w2_chunks[c] = weights.tile([P, CHUNK_PASSES, PACK, D], BF16, name="w2_chunk")
+            nc.sync.dma_start(
+                out=w2_chunks[c][:],
+                in_=Wd2[units, :].rearrange("(s p t) n -> p s t n", p=P, t=PACK),
+            )
+
+        for c in range(RING):
+            load_chunk(c)
+
+        x_sb = const.tile([P, B_TILES, D], BF16)
+        nc.sync.dma_start(out=x_sb[:], in_=x.rearrange("(m p) d -> p m d", p=P))
+        bd2_all = const.tile([P, D], BF16)
+        nc.sync.dma_start(out=bd2_all[:], in_=bd2.partition_broadcast(P))
+
+        ident = const.tile([P, P], BF16)
+        make_identity(nc, ident[:])
+        ident_f32 = const.tile([P, P], F32)
+        make_identity(nc, ident_f32[:])
+
+        zT_ps = psum.tile([P, B], BF16, tag="work")
+        for m in range(B_TILES):
+            nc.tensor.transpose(zT_ps[:, m * P : (m + 1) * P], z_sb[:, m, :], ident[:])
+        zT = const.tile([P, B], BF16)
+        nc.vector.tensor_copy(out=zT[:], in_=zT_ps[:])
+
+        bias_ps = psum.tile([P, PACK, P], BF16, tag="work")
+        bd1_by_place = bd1_rows[:].rearrange("g (p t) -> g t p", t=PACK)
+        for t in range(PACK):
+            nc.tensor.transpose(bias_ps[:, t, :], bd1_by_place[:, t, :], ident[:])
+        bias1 = const.tile([P, PACK, PASSES], F32)
+        nc.vector.tensor_copy(out=bias1[:], in_=bias_ps[:, :, 0:PASSES])
+
+        result = const.tile([P, P], F32)
+        nc.vector.memset(result[:], 0.0)
+
+        hd_rows = {}
+        hd_grouped = {}
+        w2_grouped = {}
+        hd_packed = {}
+        w2_packed = {}
+
+        def hidden_layer(g):
+            w1_by_place = w1_chunks[g // CHUNK_PASSES][:, g % CHUNK_PASSES, :].rearrange(
+                "l (p t) -> l t p", t=PACK
+            )
+            banks = []
+            for half in range(2):
+                bank = psum.tile([P, 2, B], F32, name="hid", tag="work")
+                for j in range(2):
+                    nc.tensor.matmul(
+                        out=bank[:, j, :],
+                        lhsT=w1_by_place[:, 2 * half + j, :],
+                        rhs=zT[:],
+                        start=True,
+                        stop=True,
+                    )
+                banks.append(bank)
+            hd_rows[g] = stage.tile([P, PACK, B], BF16, name="hd_rows")
+            for t in range(PACK):
+                nc.scalar.activation(
+                    out=hd_rows[g][:, t, :],
+                    in_=banks[t // 2][:, t % 2, :],
+                    func=ACT.Relu,
+                    bias=bias1[:, t, g : g + 1],
+                    scale=1.0,
+                )
+
+        def regroup_w2(g):
+            rows = w2_chunks[g // CHUNK_PASSES][:, g % CHUNK_PASSES, :, :]
+            w2_grouped[g] = stage.tile([P, D, PACK], BF16, name="w2_grouped", align_bytes=64)
+            regroup(
+                nc.scalar.copy,
+                w2_grouped[g][:, W2_COLS_VECTOR:D, :],
+                rows[:, :, W2_COLS_VECTOR:D],
+            )
+            regroup(
+                nc.vector.tensor_copy,
+                w2_grouped[g][:, 0:W2_COLS_VECTOR, :],
+                rows[:, :, 0:W2_COLS_VECTOR],
+            )
+
+        def regroup_hd(g):
+            hd_grouped[g] = stage.tile([P, B, PACK], BF16, name="hd_grouped", align_bytes=64)
+            regroup(nc.vector.tensor_copy, hd_grouped[g][:], hd_rows[g][:])
+
+        def quantise(grouped, width, name):
+            codes = packed.tile([P, width], U32, name=name + "_codes", align_bytes=64)
+            scales = packed.tile([P, width], U8, name=name + "_scales", align_bytes=64)
+            nc.vector.quantize_mx(
+                out=codes[:].bitcast(FP8X4),
+                scales=scales[:],
+                in_=grouped[:].rearrange("p c t -> p (c t)"),
+            )
+            return codes, scales
+
+        acc = [psum_acc.tile([P, D], F32, name="acc%d" % m) for m in range(B_TILES)]
+
+        def output_layer(g):
+            hd_codes, hd_scales = hd_packed[g]
+            w2_codes, w2_scales = w2_packed[g]
+            for m in range(B_TILES):
+                rows_m = slice(m * P, (m + 1) * P)
+                nc.tensor.matmul_mx(
+                    out=acc[m][:],
+                    lhsT=hd_codes[:, rows_m].bitcast(FP8X4),
+                    lhsT_scale=hd_scales[:, rows_m],
+                    rhs=w2_codes[:].bitcast(FP8X4),
+                    rhs_scale=w2_scales[:],
+                    start=(g == 0),
+                    stop=(g == PASSES - 1),
+                )
+
+        for i in range(-2, PASSES):
+            if i + 2 < PASSES:
+                hidden_layer(i + 2)
+            if 0 <= i + 1 < PASSES:
+                regroup_w2(i + 1)
+            if i >= 0:
+                hd_packed[i] = quantise(hd_grouped[i], B, "hd")
+            if 0 <= i + 1 < PASSES:
+                regroup_hd(i + 1)
+            if i >= 0:
+                w2_packed[i] = quantise(w2_grouped[i], D, "w2")
+                output_layer(i)
+            if i + 1 >= 0 and (i + 2) % CHUNK_PASSES == 0:
+                next_chunk = (i + 1) // CHUNK_PASSES + RING
+                if next_chunk < CHUNKS:
+                    load_chunk(next_chunk)
+
+        xv_sum = const.tile([P, B_TILES], F32)
+        abs_sum = const.tile([P, B_TILES], F32)
+        log_sum = const.tile([P, B_TILES], F32)
+        decay = []
+        for m in range(B_TILES):
+            v = tail.tile([P, D], F32, name="v")
+            nc.vector.tensor_tensor(out=v[:], in0=acc[m][:], in1=bd2_all[:], op=ALU.add)
+            abs_v = tail.tile([P, D], F32, name="abs_v")
+            nc.scalar.activation(
+                out=abs_v[:], in_=v[:], func=ACT.Abs, accum_out=abs_sum[:, m : m + 1]
+            )
+            decay.append(tail.tile([P, D], F32, name="decay"))
+            nc.scalar.activation(out=decay[m][:], in_=abs_v[:], func=ACT.Exp, scale=-1.0)
+            xv = tail.tile([P, D], F32, name="xv")
+            nc.vector.scalar_tensor_tensor(
+                out=xv[:],
+                in0=x_sb[:, m, :],
+                scalar=-0.5,
+                in1=v[:],
+                op0=ALU.add,
+                op1=ALU.mult,
+                accum_out=xv_sum[:, m : m + 1],
+            )
+        for m in range(B_TILES):
+            log_term = tail.tile([P, D], F32, name="log_term")
+            nc.scalar.activation(
+                out=log_term[:],
+                in_=decay[m][:],
+                func=ACT.Ln,
+                bias=1.0,
+                accum_out=log_sum[:, m : m + 1],
+            )
+
+        partial = const.tile([P, B_TILES], F32)
+        nc.vector.scalar_tensor_tensor(
+            out=partial[:], in0=abs_sum[:], scalar=-0.5, in1=xv_sum[:], op0=ALU.mult, op1=ALU.add
+        )
+        nc.vector.tensor_tensor(
+            out=result[:, 0:B_TILES], in0=partial[:], in1=log_sum[:], op=ALU.subtract
+        )
+        resultT_ps = psum.tile([P, P], F32, tag="work")
+        nc.tensor.transpose(resultT_ps[:], result[:], ident_f32[:])
+        resultT = const.tile([P, P], F32)
+        nc.vector.tensor_copy(out=resultT[:], in_=resultT_ps[:])
+        nc.sync.dma_start(out=out.rearrange("(m p) -> m p", p=P), in_=resultT[0:B_TILES, :])

@@ -19,9 +19,9 @@ B, D, L, H = 256, 512, 128, 16384
 PASSES = H // K_PASS
 B_TILES = B // P
 
-CHUNK_PASSES = 2
-CHUNKS = PASSES // CHUNK_PASSES
-RING = 8
+W1_LOAD_PASSES = 2
+W1_LOADS = PASSES // W1_LOAD_PASSES
+W2_RING = 16
 
 W2_COLS_SCALAR = 208
 W2_COLS_VECTOR = D - W2_COLS_SCALAR
@@ -40,8 +40,9 @@ def tile_vae_pb_k_kernel(tc, z, x, Wd1, bd1, Wd2, bd2, out):
     nc = tc.nc
     with ExitStack() as ctx:
         const = ctx.enter_context(tc.tile_pool(name="const", bufs=1))
-        weights = ctx.enter_context(tc.tile_pool(name="weights", bufs=RING))
-        stage = ctx.enter_context(tc.tile_pool(name="stage", bufs=3))
+        w1_pool = ctx.enter_context(tc.tile_pool(name="w1_pool", bufs=W1_LOADS))
+        w2_pool = ctx.enter_context(tc.tile_pool(name="w2_pool", bufs=W2_RING))
+        stage = ctx.enter_context(tc.tile_pool(name="stage", bufs=4))
         packed = ctx.enter_context(tc.tile_pool(name="packed", bufs=3))
         tail = ctx.enter_context(tc.tile_pool(name="tail", bufs=2))
         psum_acc = ctx.enter_context(tc.psum_pool(name="psum_acc", bufs=1))
@@ -53,23 +54,27 @@ def tile_vae_pb_k_kernel(tc, z, x, Wd1, bd1, Wd2, bd2, out):
         nc.vector.memset(bd1_rows[:], 0.0)
         nc.sync.dma_start(out=bd1_rows[0:PASSES, :], in_=bd1.rearrange("(g k) -> g k", k=K_PASS))
 
-        w1_chunks = {}
-        w2_chunks = {}
+        w1_loaded = {}
+        w2_rows = {}
 
-        def load_chunk(c):
-            units = slice(c * CHUNK_PASSES * K_PASS, (c + 1) * CHUNK_PASSES * K_PASS)
-            w1_chunks[c] = weights.tile([P, CHUNK_PASSES, K_PASS], BF16, name="w1_chunk")
+        def load_weights(g):
+            w2_rows[g] = w2_pool.tile([P, PACK, D], BF16, name="w2_rows")
             nc.sync.dma_start(
-                out=w1_chunks[c][:], in_=Wd1[:, units].rearrange("l (s k) -> l s k", k=K_PASS)
+                out=w2_rows[g][:],
+                in_=Wd2[g * K_PASS : (g + 1) * K_PASS, :].rearrange("(p t) n -> p t n", t=PACK),
             )
-            w2_chunks[c] = weights.tile([P, CHUNK_PASSES, PACK, D], BF16, name="w2_chunk")
-            nc.sync.dma_start(
-                out=w2_chunks[c][:],
-                in_=Wd2[units, :].rearrange("(s p t) n -> p s t n", p=P, t=PACK),
-            )
+            if g % W1_LOAD_PASSES == 0:
+                w1_tile = w1_pool.tile([P, W1_LOAD_PASSES, K_PASS], BF16, name="w1_tile")
+                nc.sync.dma_start(
+                    out=w1_tile[:],
+                    in_=Wd1[:, g * K_PASS : (g + W1_LOAD_PASSES) * K_PASS].rearrange(
+                        "l (s k) -> l s k", k=K_PASS
+                    ),
+                )
+                w1_loaded[g // W1_LOAD_PASSES] = w1_tile
 
-        for c in range(RING):
-            load_chunk(c)
+        for g in range(W2_RING):
+            load_weights(g)
 
         x_sb = const.tile([P, B_TILES, D], BF16)
         nc.sync.dma_start(out=x_sb[:], in_=x.rearrange("(m p) d -> p m d", p=P))
@@ -104,7 +109,7 @@ def tile_vae_pb_k_kernel(tc, z, x, Wd1, bd1, Wd2, bd2, out):
         w2_packed = {}
 
         def hidden_layer(g):
-            w1_by_place = w1_chunks[g // CHUNK_PASSES][:, g % CHUNK_PASSES, :].rearrange(
+            w1_by_place = w1_loaded[g // W1_LOAD_PASSES][:, g % W1_LOAD_PASSES, :].rearrange(
                 "l (p t) -> l t p", t=PACK
             )
             banks = []
@@ -130,7 +135,7 @@ def tile_vae_pb_k_kernel(tc, z, x, Wd1, bd1, Wd2, bd2, out):
                 )
 
         def regroup_w2(g):
-            rows = w2_chunks[g // CHUNK_PASSES][:, g % CHUNK_PASSES, :, :]
+            rows = w2_rows[g]
             w2_grouped[g] = stage.tile([P, D, PACK], BF16, name="w2_grouped", align_bytes=64)
             regroup(
                 nc.scalar.copy,
@@ -176,9 +181,10 @@ def tile_vae_pb_k_kernel(tc, z, x, Wd1, bd1, Wd2, bd2, out):
 
         for i in range(-2, PASSES):
             if i + 2 < PASSES:
+                regroup_w2(i + 2)
+                if i + 2 + W2_RING < PASSES:
+                    load_weights(i + 2 + W2_RING)
                 hidden_layer(i + 2)
-            if 0 <= i + 1 < PASSES:
-                regroup_w2(i + 1)
             if i >= 0:
                 hd_packed[i] = quantise(hd_grouped[i], B, "hd")
             if 0 <= i + 1 < PASSES:
@@ -186,30 +192,29 @@ def tile_vae_pb_k_kernel(tc, z, x, Wd1, bd1, Wd2, bd2, out):
             if i >= 0:
                 w2_packed[i] = quantise(w2_grouped[i], D, "w2")
                 output_layer(i)
-            if i + 1 >= 0 and (i + 2) % CHUNK_PASSES == 0:
-                next_chunk = (i + 1) // CHUNK_PASSES + RING
-                if next_chunk < CHUNKS:
-                    load_chunk(next_chunk)
 
         xv_sum = const.tile([P, B_TILES], F32)
         abs_sum = const.tile([P, B_TILES], F32)
         log_sum = const.tile([P, B_TILES], F32)
+        logits = []
         decay = []
         for m in range(B_TILES):
-            v = tail.tile([P, D], F32, name="v")
-            nc.vector.tensor_tensor(out=v[:], in0=acc[m][:], in1=bd2_all[:], op=ALU.add)
+            logits.append(tail.tile([P, D], F32, name="logits"))
+            nc.vector.tensor_tensor(out=logits[m][:], in0=acc[m][:], in1=bd2_all[:], op=ALU.add)
+        for m in range(B_TILES):
             abs_v = tail.tile([P, D], F32, name="abs_v")
             nc.scalar.activation(
-                out=abs_v[:], in_=v[:], func=ACT.Abs, accum_out=abs_sum[:, m : m + 1]
+                out=abs_v[:], in_=logits[m][:], func=ACT.Abs, accum_out=abs_sum[:, m : m + 1]
             )
             decay.append(tail.tile([P, D], F32, name="decay"))
             nc.scalar.activation(out=decay[m][:], in_=abs_v[:], func=ACT.Exp, scale=-1.0)
+        for m in range(B_TILES):
             xv = tail.tile([P, D], F32, name="xv")
             nc.vector.scalar_tensor_tensor(
                 out=xv[:],
                 in0=x_sb[:, m, :],
                 scalar=-0.5,
-                in1=v[:],
+                in1=logits[m][:],
                 op0=ALU.add,
                 op1=ALU.mult,
                 accum_out=xv_sum[:, m : m + 1],

@@ -23,7 +23,7 @@ W1_LOAD_PASSES = 2
 W1_LOADS = PASSES // W1_LOAD_PASSES
 W2_RING = 16
 
-W2_COLS_SCALAR = 208
+W2_COLS_SCALAR = 192
 W2_COLS_VECTOR = D - W2_COLS_SCALAR
 
 FLOPS = 2 * B * L * H + 2 * B * H * D
@@ -47,6 +47,7 @@ def tile_vae_pb_k_kernel(tc, z, x, Wd1, bd1, Wd2, bd2, out):
         tail = ctx.enter_context(tc.tile_pool(name="tail", bufs=2))
         psum_acc = ctx.enter_context(tc.psum_pool(name="psum_acc", bufs=1))
         psum = ctx.enter_context(tc.psum_pool(name="psum", bufs=6))
+        ctx.enter_context(tc.manual_schedule())
 
         z_sb = const.tile([P, B_TILES, L], BF16)
         nc.sync.dma_start(out=z_sb[:], in_=z.rearrange("(m p) l -> p m l", p=P))
@@ -102,17 +103,18 @@ def tile_vae_pb_k_kernel(tc, z, x, Wd1, bd1, Wd2, bd2, out):
         result = const.tile([P, P], F32)
         nc.vector.memset(result[:], 0.0)
 
+        hid_banks = {}
         hd_rows = {}
         hd_grouped = {}
         w2_grouped = {}
         hd_packed = {}
         w2_packed = {}
 
-        def hidden_layer(g):
+        def hidden_matmuls(g):
             w1_by_place = w1_loaded[g // W1_LOAD_PASSES][:, g % W1_LOAD_PASSES, :].rearrange(
                 "l (p t) -> l t p", t=PACK
             )
-            banks = []
+            hid_banks[g] = []
             for half in range(2):
                 bank = psum.tile([P, 2, B], F32, name="hid", tag="work")
                 for j in range(2):
@@ -123,12 +125,14 @@ def tile_vae_pb_k_kernel(tc, z, x, Wd1, bd1, Wd2, bd2, out):
                         start=True,
                         stop=True,
                     )
-                banks.append(bank)
+                hid_banks[g].append(bank)
+
+        def hidden_relu(g):
             hd_rows[g] = stage.tile([P, PACK, B], BF16, name="hd_rows")
             for t in range(PACK):
                 nc.scalar.activation(
                     out=hd_rows[g][:, t, :],
-                    in_=banks[t // 2][:, t % 2, :],
+                    in_=hid_banks[g][t // 2][:, t % 2, :],
                     func=ACT.Relu,
                     bias=bias1[:, t, g : g + 1],
                     scale=1.0,
@@ -179,19 +183,20 @@ def tile_vae_pb_k_kernel(tc, z, x, Wd1, bd1, Wd2, bd2, out):
                     stop=(g == PASSES - 1),
                 )
 
-        for i in range(-2, PASSES):
-            if i + 2 < PASSES:
+        for i in range(-3, PASSES):
+            if i + 3 < PASSES:
+                hidden_matmuls(i + 3)
+            if 0 <= i + 2 < PASSES:
                 regroup_w2(i + 2)
                 if i + 2 + W2_RING < PASSES:
                     load_weights(i + 2 + W2_RING)
-                hidden_layer(i + 2)
-            if i >= 0:
-                hd_packed[i] = quantise(hd_grouped[i], B, "hd")
-            if 0 <= i + 1 < PASSES:
-                regroup_hd(i + 1)
+                hidden_relu(i + 2)
             if i >= 0:
                 w2_packed[i] = quantise(w2_grouped[i], D, "w2")
+                hd_packed[i] = quantise(hd_grouped[i], B, "hd")
                 output_layer(i)
+            if 0 <= i + 1 < PASSES:
+                regroup_hd(i + 1)
 
         xv_sum = const.tile([P, B_TILES], F32)
         abs_sum = const.tile([P, B_TILES], F32)

@@ -23,8 +23,10 @@ W1_LOAD_PASSES = 2
 W1_LOADS = PASSES // W1_LOAD_PASSES
 W2_RING = 16
 
-W2_COLS_SCALAR = 192
-W2_COLS_VECTOR = D - W2_COLS_SCALAR
+ALIGNED = tuple(range(1, 30, 3))
+
+W2_COLS_SCALAR = 224
+W2_COLS_SCALAR_ALIGNED = 144
 
 FLOPS = 2 * B * L * H + 2 * B * H * D
 
@@ -52,8 +54,15 @@ def tile_vae_pb_k_kernel(tc, z, x, Wd1, bd1, Wd2, bd2, out):
         z_sb = const.tile([P, B_TILES, L], BF16)
         nc.sync.dma_start(out=z_sb[:], in_=z.rearrange("(m p) l -> p m l", p=P))
         bd1_rows = const.tile([P, K_PASS], BF16)
+        bias_rows = const.tile([P, K_PASS], BF16)
         nc.vector.memset(bd1_rows[:], 0.0)
-        nc.sync.dma_start(out=bd1_rows[0:PASSES, :], in_=bd1.rearrange("(g k) -> g k", k=K_PASS))
+        nc.vector.memset(bias_rows[:], 0.0)
+        for rows in (
+            bd1_rows[0:PASSES, :],
+            bd1_rows[PASSES : 2 * PASSES, :],
+            bias_rows[0:PASSES, :],
+        ):
+            nc.sync.dma_start(out=rows, in_=bd1.rearrange("(g k) -> g k", k=K_PASS))
 
         w1_loaded = {}
         w2_rows = {}
@@ -86,6 +95,19 @@ def tile_vae_pb_k_kernel(tc, z, x, Wd1, bd1, Wd2, bd2, out):
         make_identity(nc, ident[:])
         ident_f32 = const.tile([P, P], F32)
         make_identity(nc, ident_f32[:])
+        signs = const.tile([P, PASSES], BF16)
+        nc.vector.tensor_tensor(
+            out=signs[:], in0=ident[:, 0:PASSES], in1=ident[:, PASSES : 2 * PASSES], op=ALU.subtract
+        )
+        pick = const.tile([P, len(ALIGNED), P], BF16)
+        nc.vector.tensor_copy(
+            out=pick[:],
+            in_=signs[:, ALIGNED[0] : ALIGNED[-1] + 1 : 3]
+            .unsqueeze(2)
+            .to_broadcast([P, len(ALIGNED), P]),
+        )
+        result = const.tile([P, P], F32)
+        nc.gpsimd.memset(result[:], 0.0)
 
         zT_ps = psum.tile([P, B], BF16, tag="work")
         for m in range(B_TILES):
@@ -100,8 +122,12 @@ def tile_vae_pb_k_kernel(tc, z, x, Wd1, bd1, Wd2, bd2, out):
         bias1 = const.tile([P, PACK, PASSES], F32)
         nc.vector.tensor_copy(out=bias1[:], in_=bias_ps[:, :, 0:PASSES])
 
-        result = const.tile([P, P], F32)
-        nc.vector.memset(result[:], 0.0)
+        nc.vector.tensor_copy(
+            out=bias_rows[PASSES : 2 * PASSES, :].rearrange("g (p t) -> g p t", t=PACK),
+            in_=bd1_rows[PASSES : 2 * PASSES, :]
+            .rearrange("g (p t) -> g p t", t=PACK)[:, :, 0:1]
+            .to_broadcast([PASSES, P, PACK]),
+        )
 
         hid_banks = {}
         hd_rows = {}
@@ -127,6 +153,44 @@ def tile_vae_pb_k_kernel(tc, z, x, Wd1, bd1, Wd2, bd2, out):
                     )
                 hid_banks[g].append(bank)
 
+        bias_by_place = bias_rows[:].rearrange("g (p t) -> g t p", t=PACK)
+
+        def hidden_matmuls_aligned(g):
+            w1_by_place = w1_loaded[g // W1_LOAD_PASSES][:, g % W1_LOAD_PASSES, :].rearrange(
+                "l (p t) -> l t p", t=PACK
+            )
+            hid_banks[g] = [
+                psum.tile([P, PACK, P], F32, name="hid", tag="work") for m in range(B_TILES)
+            ]
+            for t in range(PACK):
+                for m in range(B_TILES):
+                    nc.tensor.matmul(
+                        out=hid_banks[g][m][:, t, :],
+                        lhsT=w1_by_place[:, t, :],
+                        rhs=zT[:, m * P : (m + 1) * P],
+                        start=True,
+                        stop=(t == 0),
+                    )
+                    if t > 0:
+                        nc.tensor.matmul(
+                            out=hid_banks[g][m][:, t, :],
+                            lhsT=bias_by_place[:, t, :],
+                            rhs=pick[:, ALIGNED.index(g), :],
+                            start=False,
+                            stop=True,
+                        )
+
+        def hidden_relu_aligned(g):
+            hd_grouped[g] = stage.tile([P, B, PACK], BF16, name="hd_grouped", align_bytes=64)
+            for m in range(B_TILES):
+                nc.scalar.activation(
+                    out=hd_grouped[g][:, m * P : (m + 1) * P, :],
+                    in_=hid_banks[g][m][:].rearrange("p t b -> p b t"),
+                    func=ACT.Relu,
+                    bias=bias1[:, 0, g : g + 1],
+                    scale=1.0,
+                )
+
         def hidden_relu(g):
             hd_rows[g] = stage.tile([P, PACK, B], BF16, name="hd_rows")
             for t in range(PACK):
@@ -140,16 +204,17 @@ def tile_vae_pb_k_kernel(tc, z, x, Wd1, bd1, Wd2, bd2, out):
 
         def regroup_w2(g):
             rows = w2_rows[g]
+            v_cols = D - (W2_COLS_SCALAR_ALIGNED if g in ALIGNED else W2_COLS_SCALAR)
             w2_grouped[g] = stage.tile([P, D, PACK], BF16, name="w2_grouped", align_bytes=64)
             regroup(
                 nc.scalar.copy,
-                w2_grouped[g][:, W2_COLS_VECTOR:D, :],
-                rows[:, :, W2_COLS_VECTOR:D],
+                w2_grouped[g][:, v_cols:D, :],
+                rows[:, :, v_cols:D],
             )
             regroup(
                 nc.vector.tensor_copy,
-                w2_grouped[g][:, 0:W2_COLS_VECTOR, :],
-                rows[:, :, 0:W2_COLS_VECTOR],
+                w2_grouped[g][:, 0:v_cols, :],
+                rows[:, :, 0:v_cols],
             )
 
         def regroup_hd(g):
@@ -185,17 +250,17 @@ def tile_vae_pb_k_kernel(tc, z, x, Wd1, bd1, Wd2, bd2, out):
 
         for i in range(-3, PASSES):
             if i + 3 < PASSES:
-                hidden_matmuls(i + 3)
+                (hidden_matmuls_aligned if i + 3 in ALIGNED else hidden_matmuls)(i + 3)
             if 0 <= i + 2 < PASSES:
                 regroup_w2(i + 2)
                 if i + 2 + W2_RING < PASSES:
                     load_weights(i + 2 + W2_RING)
-                hidden_relu(i + 2)
+                (hidden_relu_aligned if i + 2 in ALIGNED else hidden_relu)(i + 2)
             if i >= 0:
                 w2_packed[i] = quantise(w2_grouped[i], D, "w2")
                 hd_packed[i] = quantise(hd_grouped[i], B, "hd")
                 output_layer(i)
-            if 0 <= i + 1 < PASSES:
+            if 0 <= i + 1 < PASSES and i + 1 not in ALIGNED:
                 regroup_hd(i + 1)
 
         xv_sum = const.tile([P, B_TILES], F32)

@@ -23,7 +23,7 @@ W1_LOAD_PASSES = 2
 W1_LOADS = PASSES // W1_LOAD_PASSES
 W2_RING = 16
 
-ALIGNED = tuple(range(1, 30, 3))
+ALIGNED = tuple(range(3, 31, 3))
 
 W2_COLS_SCALAR = 224
 W2_COLS_SCALAR_ALIGNED = 144
@@ -52,17 +52,18 @@ def tile_vae_pb_k_kernel(tc, z, x, Wd1, bd1, Wd2, bd2, out):
         ctx.enter_context(tc.manual_schedule())
 
         z_sb = const.tile([P, B_TILES, L], BF16)
-        nc.sync.dma_start(out=z_sb[:], in_=z.rearrange("(m p) l -> p m l", p=P))
+        nc.scalar.dma_start(out=z_sb[:], in_=z.rearrange("(m p) l -> p m l", p=P))
         bd1_rows = const.tile([P, K_PASS], BF16)
         bias_rows = const.tile([P, K_PASS], BF16)
-        nc.vector.memset(bd1_rows[:], 0.0)
-        nc.vector.memset(bias_rows[:], 0.0)
-        for rows in (
-            bd1_rows[0:PASSES, :],
-            bd1_rows[PASSES : 2 * PASSES, :],
-            bias_rows[0:PASSES, :],
-        ):
-            nc.sync.dma_start(out=rows, in_=bd1.rearrange("(g k) -> g k", k=K_PASS))
+        for first, last in ((PASSES, 2 * PASSES), (2 * PASSES, P)):
+            nc.vector.memset(bd1_rows[first:last, :], 0.0)
+        nc.vector.memset(bias_rows[2 * PASSES : P, :], 0.0)
+        spare_rows = const.tile([P, K_PASS], BF16)
+
+        def load_bias(rows):
+            nc.scalar.dma_start(out=rows, in_=bd1.rearrange("(g k) -> g k", k=K_PASS))
+
+        load_bias(bd1_rows[0:PASSES, :])
 
         w1_loaded = {}
         w2_rows = {}
@@ -85,6 +86,8 @@ def tile_vae_pb_k_kernel(tc, z, x, Wd1, bd1, Wd2, bd2, out):
 
         for g in range(W2_RING):
             load_weights(g)
+        load_bias(bias_rows[0:PASSES, :])
+        load_bias(spare_rows[PASSES : 2 * PASSES, :])
 
         x_sb = const.tile([P, B_TILES, D], BF16)
         nc.sync.dma_start(out=x_sb[:], in_=x.rearrange("(m p) d -> p m d", p=P))
@@ -106,28 +109,20 @@ def tile_vae_pb_k_kernel(tc, z, x, Wd1, bd1, Wd2, bd2, out):
             .unsqueeze(2)
             .to_broadcast([P, len(ALIGNED), P]),
         )
-        result = const.tile([P, P], F32)
-        nc.gpsimd.memset(result[:], 0.0)
+        early_terms = const.tile([P, P], F32)
+        log_terms = const.tile([P, P], F32)
+        nc.gpsimd.memset(early_terms[:], 0.0)
+        nc.gpsimd.memset(log_terms[:], 0.0)
 
         zT_ps = psum.tile([P, B], BF16, tag="work")
         for m in range(B_TILES):
             nc.tensor.transpose(zT_ps[:, m * P : (m + 1) * P], z_sb[:, m, :], ident[:])
         zT = const.tile([P, B], BF16)
-        nc.vector.tensor_copy(out=zT[:], in_=zT_ps[:])
 
         bias_ps = psum.tile([P, PACK, P], BF16, tag="work")
         bd1_by_place = bd1_rows[:].rearrange("g (p t) -> g t p", t=PACK)
         for t in range(PACK):
             nc.tensor.transpose(bias_ps[:, t, :], bd1_by_place[:, t, :], ident[:])
-        bias1 = const.tile([P, PACK, PASSES], F32)
-        nc.vector.tensor_copy(out=bias1[:], in_=bias_ps[:, :, 0:PASSES])
-
-        nc.vector.tensor_copy(
-            out=bias_rows[PASSES : 2 * PASSES, :].rearrange("g (p t) -> g p t", t=PACK),
-            in_=bd1_rows[PASSES : 2 * PASSES, :]
-            .rearrange("g (p t) -> g p t", t=PACK)[:, :, 0:1]
-            .to_broadcast([PASSES, P, PACK]),
-        )
 
         hid_banks = {}
         hd_rows = {}
@@ -248,14 +243,31 @@ def tile_vae_pb_k_kernel(tc, z, x, Wd1, bd1, Wd2, bd2, out):
                     stop=(g == PASSES - 1),
                 )
 
+        def spread_first_place():
+            nc.vector.tensor_copy(
+                out=bias_rows[PASSES : 2 * PASSES, :].rearrange("g (p t) -> g p t", t=PACK),
+                in_=spare_rows[PASSES : 2 * PASSES, :]
+                .rearrange("g (p t) -> g p t", t=PACK)[:, :, 0:1]
+                .to_broadcast([PASSES, P, PACK]),
+            )
+
+        regroup_w2(0)
+        load_weights(W2_RING)
+        nc.vector.tensor_copy(out=zT[:], in_=zT_ps[:])
+        bias1 = const.tile([P, PACK, PASSES], F32)
+        nc.vector.tensor_copy(out=bias1[:], in_=bias_ps[:, :, 0:PASSES])
+
         for i in range(-3, PASSES):
             if i + 3 < PASSES:
                 (hidden_matmuls_aligned if i + 3 in ALIGNED else hidden_matmuls)(i + 3)
             if 0 <= i + 2 < PASSES:
-                regroup_w2(i + 2)
-                if i + 2 + W2_RING < PASSES:
-                    load_weights(i + 2 + W2_RING)
+                if i + 2 > 0:
+                    regroup_w2(i + 2)
+                    if i + 2 + W2_RING < PASSES:
+                        load_weights(i + 2 + W2_RING)
                 (hidden_relu_aligned if i + 2 in ALIGNED else hidden_relu)(i + 2)
+            if i == -1:
+                spread_first_place()
             if i >= 0:
                 w2_packed[i] = quantise(w2_grouped[i], D, "w2")
                 hd_packed[i] = quantise(hd_grouped[i], B, "hd")
@@ -265,20 +277,28 @@ def tile_vae_pb_k_kernel(tc, z, x, Wd1, bd1, Wd2, bd2, out):
 
         xv_sum = const.tile([P, B_TILES], F32)
         abs_sum = const.tile([P, B_TILES], F32)
-        log_sum = const.tile([P, B_TILES], F32)
         logits = []
-        decay = []
         for m in range(B_TILES):
             logits.append(tail.tile([P, D], F32, name="logits"))
             nc.vector.tensor_tensor(out=logits[m][:], in0=acc[m][:], in1=bd2_all[:], op=ALU.add)
+        abs_v = [tail.tile([P, D], F32, name="abs_v") for m in range(B_TILES)]
+        nc.scalar.activation(
+            out=abs_v[0][:], in_=logits[0][:], func=ACT.Abs, accum_out=abs_sum[:, 0:1]
+        )
+        nc.vector.scalar_tensor_tensor(
+            out=abs_v[1][:],
+            in0=logits[1][:],
+            scalar=-1.0,
+            in1=logits[1][:],
+            op0=ALU.mult,
+            op1=ALU.max,
+            accum_out=abs_sum[:, 1:2],
+        )
+        decay = [tail.tile([P, D], F32, name="decay") for m in range(B_TILES)]
         for m in range(B_TILES):
-            abs_v = tail.tile([P, D], F32, name="abs_v")
-            nc.scalar.activation(
-                out=abs_v[:], in_=logits[m][:], func=ACT.Abs, accum_out=abs_sum[:, m : m + 1]
-            )
-            decay.append(tail.tile([P, D], F32, name="decay"))
-            nc.scalar.activation(out=decay[m][:], in_=abs_v[:], func=ACT.Exp, scale=-1.0)
-        for m in range(B_TILES):
+            nc.scalar.activation(out=decay[m][:], in_=abs_v[m][:], func=ACT.Exp, scale=-1.0)
+
+        def cross_term(m):
             xv = tail.tile([P, D], F32, name="xv")
             nc.vector.scalar_tensor_tensor(
                 out=xv[:],
@@ -289,25 +309,59 @@ def tile_vae_pb_k_kernel(tc, z, x, Wd1, bd1, Wd2, bd2, out):
                 op1=ALU.mult,
                 accum_out=xv_sum[:, m : m + 1],
             )
-        for m in range(B_TILES):
-            log_term = tail.tile([P, D], F32, name="log_term")
-            nc.scalar.activation(
-                out=log_term[:],
-                in_=decay[m][:],
-                func=ACT.Ln,
-                bias=1.0,
-                accum_out=log_sum[:, m : m + 1],
+
+        factors = const.tile([P, B_TILES, D // 2], F32)
+
+        def multiply_factors(m):
+            upper = tail.tile([P, D // 2], F32, name="upper")
+            nc.vector.tensor_scalar_add(upper[:], decay[m][:, D // 2 : D], 1.0)
+            nc.vector.scalar_tensor_tensor(
+                out=factors[:, m, :],
+                in0=decay[m][:, 0 : D // 2],
+                scalar=1.0,
+                in1=upper[:],
+                op0=ALU.add,
+                op1=ALU.mult,
             )
 
-        partial = const.tile([P, B_TILES], F32)
+        cross_term(0)
+        multiply_factors(0)
+        multiply_factors(1)
+        cross_term(1)
         nc.vector.scalar_tensor_tensor(
-            out=partial[:], in0=abs_sum[:], scalar=-0.5, in1=xv_sum[:], op0=ALU.mult, op1=ALU.add
+            out=early_terms[:, 0:B_TILES],
+            in0=abs_sum[:],
+            scalar=0.5,
+            in1=xv_sum[:],
+            op0=ALU.mult,
+            op1=ALU.subtract,
         )
-        nc.vector.tensor_tensor(
-            out=result[:, 0:B_TILES], in0=partial[:], in1=log_sum[:], op=ALU.subtract
+        for m in range(B_TILES):
+            log_factors = tail.tile([P, D // 2], F32, name="log_factors")
+            nc.scalar.activation(
+                out=log_factors[:],
+                in_=factors[:, m, :],
+                func=ACT.Ln,
+                accum_out=log_terms[:, m : m + 1],
+            )
+
+        sums_ps = psum.tile([P, P], F32, tag="work")
+        nc.tensor.matmul(
+            out=sums_ps[:],
+            lhsT=early_terms[:],
+            rhs=ident_f32[:],
+            is_transpose=True,
+            start=True,
+            stop=False,
         )
-        resultT_ps = psum.tile([P, P], F32, tag="work")
-        nc.tensor.transpose(resultT_ps[:], result[:], ident_f32[:])
-        resultT = const.tile([P, P], F32)
-        nc.vector.tensor_copy(out=resultT[:], in_=resultT_ps[:])
-        nc.sync.dma_start(out=out.rearrange("(m p) -> m p", p=P), in_=resultT[0:B_TILES, :])
+        nc.tensor.matmul(
+            out=sums_ps[:],
+            lhsT=log_terms[:],
+            rhs=ident_f32[:],
+            is_transpose=True,
+            start=False,
+            stop=True,
+        )
+        result = const.tile([P, P], F32)
+        nc.vector.tensor_scalar_mul(result[:], sums_ps[:], -1.0)
+        nc.sync.dma_start(out=out.rearrange("(m p) -> m p", p=P), in_=result[0:B_TILES, :])

@@ -33,8 +33,8 @@ FLOPS = 2 * B * L * H + 2 * B * H * D
 
 def regroup(copy, grouped, rows):
     copy(
-        out=grouped.rearrange("p (c i) t -> p c t i", i=4),
-        in_=rows.rearrange("p t (c i) -> p c t i", i=4),
+        out=grouped.rearrange("p (c i) t -> p c t i", i=8),
+        in_=rows.rearrange("p t (c i) -> p c t i", i=8),
     )
 
 

@@ -21,20 +21,23 @@ B_TILES = B // P
 
 W1_LOAD_PASSES = 2
 W1_LOADS = PASSES // W1_LOAD_PASSES
-W2_RING = 16
 
-ALIGNED = tuple(range(3, 31, 3))
+UNITS = [[0], [1]] + [[g, g + 1] for g in range(2, PASSES - 2, 2)] + [[PASSES - 2], [PASSES - 1]]
+UNIT_MAX = 2
+W2_RING = 9
+
+ALIGNED = tuple(range(11, 31, 2))
 
 W2_COLS_SCALAR = 224
-W2_COLS_SCALAR_ALIGNED = 144
+W2_COLS_SCALAR_ALIGNED = 184
 
 FLOPS = 2 * B * L * H + 2 * B * H * D
 
 
 def regroup(copy, grouped, rows):
     copy(
-        out=grouped.rearrange("p (c i) t -> p c t i", i=8),
-        in_=rows.rearrange("p t (c i) -> p c t i", i=8),
+        out=grouped.rearrange("p s (c i) t -> p s c t i", i=8),
+        in_=rows.rearrange("p s t (c i) -> p s c t i", i=8),
     )
 
 
@@ -44,7 +47,8 @@ def tile_vae_pb_k_kernel(tc, z, x, Wd1, bd1, Wd2, bd2, out):
         const = ctx.enter_context(tc.tile_pool(name="const", bufs=1))
         w1_pool = ctx.enter_context(tc.tile_pool(name="w1_pool", bufs=W1_LOADS))
         w2_pool = ctx.enter_context(tc.tile_pool(name="w2_pool", bufs=W2_RING))
-        stage = ctx.enter_context(tc.tile_pool(name="stage", bufs=4))
+        stage = ctx.enter_context(tc.tile_pool(name="stage", bufs=3))
+        w2_stage = ctx.enter_context(tc.tile_pool(name="w2_stage", bufs=4))
         packed = ctx.enter_context(tc.tile_pool(name="packed", bufs=3))
         tail = ctx.enter_context(tc.tile_pool(name="tail", bufs=2))
         psum_acc = ctx.enter_context(tc.psum_pool(name="psum_acc", bufs=1))
@@ -68,24 +72,28 @@ def tile_vae_pb_k_kernel(tc, z, x, Wd1, bd1, Wd2, bd2, out):
         w1_loaded = {}
         w2_rows = {}
 
-        def load_weights(g):
-            w2_rows[g] = w2_pool.tile([P, PACK, D], BF16, name="w2_rows")
+        def load_weights(u):
+            passes = UNITS[u]
+            w2_rows[u] = w2_pool.tile([P, UNIT_MAX, PACK, D], BF16, name="w2_rows")
             nc.sync.dma_start(
-                out=w2_rows[g][:],
-                in_=Wd2[g * K_PASS : (g + 1) * K_PASS, :].rearrange("(p t) n -> p t n", t=PACK),
+                out=w2_rows[u][:, 0 : len(passes), :, :],
+                in_=Wd2[passes[0] * K_PASS : (passes[-1] + 1) * K_PASS, :].rearrange(
+                    "(s p t) n -> p s t n", p=P, t=PACK
+                ),
             )
-            if g % W1_LOAD_PASSES == 0:
-                w1_tile = w1_pool.tile([P, W1_LOAD_PASSES, K_PASS], BF16, name="w1_tile")
-                nc.sync.dma_start(
-                    out=w1_tile[:],
-                    in_=Wd1[:, g * K_PASS : (g + W1_LOAD_PASSES) * K_PASS].rearrange(
-                        "l (s k) -> l s k", k=K_PASS
-                    ),
-                )
-                w1_loaded[g // W1_LOAD_PASSES] = w1_tile
+            for g in passes:
+                if g % W1_LOAD_PASSES == 0:
+                    w1_tile = w1_pool.tile([P, W1_LOAD_PASSES, K_PASS], BF16, name="w1_tile")
+                    nc.sync.dma_start(
+                        out=w1_tile[:],
+                        in_=Wd1[:, g * K_PASS : (g + W1_LOAD_PASSES) * K_PASS].rearrange(
+                            "l (s k) -> l s k", k=K_PASS
+                        ),
+                    )
+                    w1_loaded[g // W1_LOAD_PASSES] = w1_tile
 
-        for g in range(W2_RING):
-            load_weights(g)
+        for u in range(W2_RING):
+            load_weights(u)
         load_bias(bias_rows[0:PASSES, :])
         load_bias(spare_rows[PASSES : 2 * PASSES, :])
 
@@ -105,7 +113,7 @@ def tile_vae_pb_k_kernel(tc, z, x, Wd1, bd1, Wd2, bd2, out):
         pick = const.tile([P, len(ALIGNED), P], BF16)
         nc.vector.tensor_copy(
             out=pick[:],
-            in_=signs[:, ALIGNED[0] : ALIGNED[-1] + 1 : 3]
+            in_=signs[:, ALIGNED[0] : ALIGNED[-1] + 1 : 2]
             .unsqueeze(2)
             .to_broadcast([P, len(ALIGNED), P]),
         )
@@ -175,73 +183,82 @@ def tile_vae_pb_k_kernel(tc, z, x, Wd1, bd1, Wd2, bd2, out):
                             stop=True,
                         )
 
-        def hidden_relu_aligned(g):
-            hd_grouped[g] = stage.tile([P, B, PACK], BF16, name="hd_grouped", align_bytes=64)
-            for m in range(B_TILES):
-                nc.scalar.activation(
-                    out=hd_grouped[g][:, m * P : (m + 1) * P, :],
-                    in_=hid_banks[g][m][:].rearrange("p t b -> p b t"),
-                    func=ACT.Relu,
-                    bias=bias1[:, 0, g : g + 1],
-                    scale=1.0,
-                )
-
-        def hidden_relu(g):
-            hd_rows[g] = stage.tile([P, PACK, B], BF16, name="hd_rows")
-            for t in range(PACK):
-                nc.scalar.activation(
-                    out=hd_rows[g][:, t, :],
-                    in_=hid_banks[g][t // 2][:, t % 2, :],
-                    func=ACT.Relu,
-                    bias=bias1[:, t, g : g + 1],
-                    scale=1.0,
-                )
-
-        def regroup_w2(g):
-            rows = w2_rows[g]
-            v_cols = D - (W2_COLS_SCALAR_ALIGNED if g in ALIGNED else W2_COLS_SCALAR)
-            w2_grouped[g] = stage.tile([P, D, PACK], BF16, name="w2_grouped", align_bytes=64)
-            regroup(
-                nc.scalar.copy,
-                w2_grouped[g][:, v_cols:D, :],
-                rows[:, :, v_cols:D],
+        def hidden_relu(u):
+            hd_grouped[u] = stage.tile(
+                [P, UNIT_MAX, B, PACK], BF16, name="hd_grouped", align_bytes=64
             )
+            hd_rows[u] = stage.tile([P, UNIT_MAX, PACK, B], BF16, name="hd_rows")
+            for s, g in enumerate(UNITS[u]):
+                if g in ALIGNED:
+                    for m in range(B_TILES):
+                        nc.scalar.activation(
+                            out=hd_grouped[u][:, s, m * P : (m + 1) * P, :],
+                            in_=hid_banks[g][m][:].rearrange("p t b -> p b t"),
+                            func=ACT.Relu,
+                            bias=bias1[:, 0, g : g + 1],
+                            scale=1.0,
+                        )
+                else:
+                    for t in range(PACK):
+                        nc.scalar.activation(
+                            out=hd_rows[u][:, s, t, :],
+                            in_=hid_banks[g][t // 2][:, t % 2, :],
+                            func=ACT.Relu,
+                            bias=bias1[:, t, g : g + 1],
+                            scale=1.0,
+                        )
+
+        def regroup_w2(u):
+            n = len(UNITS[u])
+            aligned = any(g in ALIGNED for g in UNITS[u])
+            v_cols = D - (W2_COLS_SCALAR_ALIGNED if aligned else W2_COLS_SCALAR)
+            w2_grouped[u] = w2_stage.tile(
+                [P, UNIT_MAX, D, PACK], BF16, name="w2_grouped", align_bytes=64
+            )
+            for copy, cols in (
+                (nc.scalar.copy, slice(v_cols, D)),
+                (nc.vector.tensor_copy, slice(0, v_cols)),
+            ):
+                regroup(copy, w2_grouped[u][:, 0:n, cols, :], w2_rows[u][:, 0:n, :, cols])
+
+        def regroup_hd(u):
+            n = sum(g not in ALIGNED for g in UNITS[u])
             regroup(
-                nc.vector.tensor_copy,
-                w2_grouped[g][:, 0:v_cols, :],
-                rows[:, :, 0:v_cols],
+                nc.vector.tensor_copy, hd_grouped[u][:, 0:n, :, :], hd_rows[u][:, 0:n, :, :]
             )
 
-        def regroup_hd(g):
-            hd_grouped[g] = stage.tile([P, B, PACK], BF16, name="hd_grouped", align_bytes=64)
-            regroup(nc.vector.tensor_copy, hd_grouped[g][:], hd_rows[g][:])
-
-        def quantise(grouped, width, name):
-            codes = packed.tile([P, width], U32, name=name + "_codes", align_bytes=64)
-            scales = packed.tile([P, width], U8, name=name + "_scales", align_bytes=64)
+        def quantise(grouped, n, width, name):
+            codes = packed.tile(
+                [P, UNIT_MAX * width], U32, name=name + "_codes", align_bytes=64
+            )
+            scales = packed.tile(
+                [P, UNIT_MAX * width], U8, name=name + "_scales", align_bytes=64
+            )
             nc.vector.quantize_mx(
-                out=codes[:].bitcast(FP8X4),
-                scales=scales[:],
-                in_=grouped[:].rearrange("p c t -> p (c t)"),
+                out=codes[:, 0 : n * width].bitcast(FP8X4),
+                scales=scales[:, 0 : n * width],
+                in_=grouped[:, 0:n, :, :].rearrange("p s c t -> p (s c t)"),
             )
             return codes, scales
 
         acc = [psum_acc.tile([P, D], F32, name="acc%d" % m) for m in range(B_TILES)]
 
-        def output_layer(g):
-            hd_codes, hd_scales = hd_packed[g]
-            w2_codes, w2_scales = w2_packed[g]
-            for m in range(B_TILES):
-                rows_m = slice(m * P, (m + 1) * P)
-                nc.tensor.matmul_mx(
-                    out=acc[m][:],
-                    lhsT=hd_codes[:, rows_m].bitcast(FP8X4),
-                    lhsT_scale=hd_scales[:, rows_m],
-                    rhs=w2_codes[:].bitcast(FP8X4),
-                    rhs_scale=w2_scales[:],
-                    start=(g == 0),
-                    stop=(g == PASSES - 1),
-                )
+        def output_layer(u):
+            hd_codes, hd_scales = hd_packed[u]
+            w2_codes, w2_scales = w2_packed[u]
+            for s, g in enumerate(UNITS[u]):
+                for m in range(B_TILES):
+                    rows_m = slice(s * B + m * P, s * B + (m + 1) * P)
+                    cols = slice(s * D, (s + 1) * D)
+                    nc.tensor.matmul_mx(
+                        out=acc[m][:],
+                        lhsT=hd_codes[:, rows_m].bitcast(FP8X4),
+                        lhsT_scale=hd_scales[:, rows_m],
+                        rhs=w2_codes[:, cols].bitcast(FP8X4),
+                        rhs_scale=w2_scales[:, cols],
+                        start=(g == 0),
+                        stop=(g == PASSES - 1),
+                    )
 
         def spread_first_place():
             nc.vector.tensor_copy(
@@ -257,22 +274,24 @@ def tile_vae_pb_k_kernel(tc, z, x, Wd1, bd1, Wd2, bd2, out):
         bias1 = const.tile([P, PACK, PASSES], F32)
         nc.vector.tensor_copy(out=bias1[:], in_=bias_ps[:, :, 0:PASSES])
 
-        for i in range(-3, PASSES):
-            if i + 3 < PASSES:
-                (hidden_matmuls_aligned if i + 3 in ALIGNED else hidden_matmuls)(i + 3)
-            if 0 <= i + 2 < PASSES:
-                if i + 2 > 0:
-                    regroup_w2(i + 2)
-                    if i + 2 + W2_RING < PASSES:
-                        load_weights(i + 2 + W2_RING)
-                (hidden_relu_aligned if i + 2 in ALIGNED else hidden_relu)(i + 2)
-            if i == -1:
+        for i in range(-2, len(UNITS)):
+            if i + 2 < len(UNITS):
+                for g in UNITS[i + 2]:
+                    (hidden_matmuls_aligned if g in ALIGNED else hidden_matmuls)(g)
+            if 0 <= i + 1 < len(UNITS):
+                hidden_relu(i + 1)
+            if 0 < i + 2 < len(UNITS):
+                regroup_w2(i + 2)
+                if i + 2 + W2_RING < len(UNITS):
+                    load_weights(i + 2 + W2_RING)
+            if i == 1:
                 spread_first_place()
             if i >= 0:
-                w2_packed[i] = quantise(w2_grouped[i], D, "w2")
-                hd_packed[i] = quantise(hd_grouped[i], B, "hd")
+                n = len(UNITS[i])
+                w2_packed[i] = quantise(w2_grouped[i], n, D, "w2")
+                hd_packed[i] = quantise(hd_grouped[i], n, B, "hd")
                 output_layer(i)
-            if 0 <= i + 1 < PASSES and i + 1 not in ALIGNED:
+            if 0 <= i + 1 < len(UNITS):
                 regroup_hd(i + 1)
 
         xv_sum = const.tile([P, B_TILES], F32)

@@ -26,10 +26,12 @@ UNITS = [[0], [1]] + [[g, g + 1] for g in range(2, PASSES - 2, 2)] + [[PASSES - 
 UNIT_MAX = 2
 W2_RING = 9
 
-ALIGNED = tuple(range(11, 31, 2))
+ODD_OF_PAIR = tuple(range(3, PASSES - 2, 2))
+ALIGNED = [g for g in ODD_OF_PAIR if g % 8 != 3]
 
 W2_COLS_SCALAR = 224
 W2_COLS_SCALAR_ALIGNED = 184
+W2_COLS_SHIFT = 48
 
 FLOPS = 2 * B * L * H + 2 * B * H * D
 
@@ -56,7 +58,7 @@ def tile_vae_pb_k_kernel(tc, z, x, Wd1, bd1, Wd2, bd2, out):
         ctx.enter_context(tc.manual_schedule())
 
         z_sb = const.tile([P, B_TILES, L], BF16)
-        nc.scalar.dma_start(out=z_sb[:], in_=z.rearrange("(m p) l -> p m l", p=P))
+        nc.sync.dma_start(out=z_sb[:], in_=z.rearrange("(m p) l -> p m l", p=P))
         bd1_rows = const.tile([P, K_PASS], BF16)
         bias_rows = const.tile([P, K_PASS], BF16)
         for first, last in ((PASSES, 2 * PASSES), (2 * PASSES, P)):
@@ -110,12 +112,12 @@ def tile_vae_pb_k_kernel(tc, z, x, Wd1, bd1, Wd2, bd2, out):
         nc.vector.tensor_tensor(
             out=signs[:], in0=ident[:, 0:PASSES], in1=ident[:, PASSES : 2 * PASSES], op=ALU.subtract
         )
-        pick = const.tile([P, len(ALIGNED), P], BF16)
+        pick = const.tile([P, len(ODD_OF_PAIR), P], BF16)
         nc.vector.tensor_copy(
             out=pick[:],
-            in_=signs[:, ALIGNED[0] : ALIGNED[-1] + 1 : 2]
+            in_=signs[:, ODD_OF_PAIR[0] : ODD_OF_PAIR[-1] + 1 : 2]
             .unsqueeze(2)
-            .to_broadcast([P, len(ALIGNED), P]),
+            .to_broadcast([P, len(ODD_OF_PAIR), P]),
         )
         early_terms = const.tile([P, P], F32)
         log_terms = const.tile([P, P], F32)
@@ -178,7 +180,7 @@ def tile_vae_pb_k_kernel(tc, z, x, Wd1, bd1, Wd2, bd2, out):
                         nc.tensor.matmul(
                             out=hid_banks[g][m][:, t, :],
                             lhsT=bias_by_place[:, t, :],
-                            rhs=pick[:, ALIGNED.index(g), :],
+                            rhs=pick[:, ODD_OF_PAIR.index(g), :],
                             start=False,
                             stop=True,
                         )
@@ -211,7 +213,9 @@ def tile_vae_pb_k_kernel(tc, z, x, Wd1, bd1, Wd2, bd2, out):
         def regroup_w2(u):
             n = len(UNITS[u])
             aligned = any(g in ALIGNED for g in UNITS[u])
-            v_cols = D - (W2_COLS_SCALAR_ALIGNED if aligned else W2_COLS_SCALAR)
+            s_cols = W2_COLS_SCALAR_ALIGNED if aligned else W2_COLS_SCALAR
+            s_cols += W2_COLS_SHIFT * (3 * u // len(UNITS) - 1)
+            v_cols = D - s_cols
             w2_grouped[u] = w2_stage.tile(
                 [P, UNIT_MAX, D, PACK], BF16, name="w2_grouped", align_bytes=64
             )
@@ -268,9 +272,9 @@ def tile_vae_pb_k_kernel(tc, z, x, Wd1, bd1, Wd2, bd2, out):
                 .to_broadcast([PASSES, P, PACK]),
             )
 
+        nc.vector.tensor_copy(out=zT[:], in_=zT_ps[:])
         regroup_w2(0)
         load_weights(W2_RING)
-        nc.vector.tensor_copy(out=zT[:], in_=zT_ps[:])
         bias1 = const.tile([P, PACK, PASSES], F32)
         nc.vector.tensor_copy(out=bias1[:], in_=bias_ps[:, :, 0:PASSES])
 
@@ -280,17 +284,17 @@ def tile_vae_pb_k_kernel(tc, z, x, Wd1, bd1, Wd2, bd2, out):
                     (hidden_matmuls_aligned if g in ALIGNED else hidden_matmuls)(g)
             if 0 <= i + 1 < len(UNITS):
                 hidden_relu(i + 1)
-            if 0 < i + 2 < len(UNITS):
-                regroup_w2(i + 2)
-                if i + 2 + W2_RING < len(UNITS):
-                    load_weights(i + 2 + W2_RING)
-            if i == 1:
+            if i == 0:
                 spread_first_place()
             if i >= 0:
                 n = len(UNITS[i])
                 w2_packed[i] = quantise(w2_grouped[i], n, D, "w2")
                 hd_packed[i] = quantise(hd_grouped[i], n, B, "hd")
                 output_layer(i)
+            if 0 < i + 2 < len(UNITS):
+                regroup_w2(i + 2)
+                if i + 2 + W2_RING < len(UNITS):
+                    load_weights(i + 2 + W2_RING)
             if 0 <= i + 1 < len(UNITS):
                 regroup_hd(i + 1)
 

@@ -26,11 +26,10 @@ UNITS = [[0], [1]] + [[g, g + 1] for g in range(2, PASSES - 2, 2)] + [[PASSES - 
 UNIT_MAX = 2
 W2_RING = 9
 
-ODD_OF_PAIR = tuple(range(3, PASSES - 2, 2))
-ALIGNED = [g for g in ODD_OF_PAIR if g % 8 != 3]
+ALIGNED = [g for g in range(5, PASSES, 2) if g // 2 % 3 != 1]
 
 W2_COLS_SCALAR = 224
-W2_COLS_SCALAR_ALIGNED = 184
+W2_COLS_ALIGNED = 80
 W2_COLS_SHIFT = 48
 
 FLOPS = 2 * B * L * H + 2 * B * H * D
@@ -112,12 +111,12 @@ def tile_vae_pb_k_kernel(tc, z, x, Wd1, bd1, Wd2, bd2, out):
         nc.vector.tensor_tensor(
             out=signs[:], in0=ident[:, 0:PASSES], in1=ident[:, PASSES : 2 * PASSES], op=ALU.subtract
         )
-        pick = const.tile([P, len(ODD_OF_PAIR), P], BF16)
+        pick = const.tile([P, PASSES // 2, P], BF16)
         nc.vector.tensor_copy(
             out=pick[:],
-            in_=signs[:, ODD_OF_PAIR[0] : ODD_OF_PAIR[-1] + 1 : 2]
+            in_=signs[:, 1:PASSES:2]
             .unsqueeze(2)
-            .to_broadcast([P, len(ODD_OF_PAIR), P]),
+            .to_broadcast([P, PASSES // 2, P]),
         )
         early_terms = const.tile([P, P], F32)
         log_terms = const.tile([P, P], F32)
@@ -180,7 +179,7 @@ def tile_vae_pb_k_kernel(tc, z, x, Wd1, bd1, Wd2, bd2, out):
                         nc.tensor.matmul(
                             out=hid_banks[g][m][:, t, :],
                             lhsT=bias_by_place[:, t, :],
-                            rhs=pick[:, ODD_OF_PAIR.index(g), :],
+                            rhs=pick[:, g // 2, :],
                             start=False,
                             stop=True,
                         )
@@ -189,7 +188,8 @@ def tile_vae_pb_k_kernel(tc, z, x, Wd1, bd1, Wd2, bd2, out):
             hd_grouped[u] = stage.tile(
                 [P, UNIT_MAX, B, PACK], BF16, name="hd_grouped", align_bytes=64
             )
-            hd_rows[u] = stage.tile([P, UNIT_MAX, PACK, B], BF16, name="hd_rows")
+            if UNITS[u][0] not in ALIGNED:
+                hd_rows[u] = stage.tile([P, UNIT_MAX, PACK, B], BF16, name="hd_rows")
             for s, g in enumerate(UNITS[u]):
                 if g in ALIGNED:
                     for m in range(B_TILES):
@@ -212,8 +212,8 @@ def tile_vae_pb_k_kernel(tc, z, x, Wd1, bd1, Wd2, bd2, out):
 
         def regroup_w2(u):
             n = len(UNITS[u])
-            aligned = any(g in ALIGNED for g in UNITS[u])
-            s_cols = W2_COLS_SCALAR_ALIGNED if aligned else W2_COLS_SCALAR
+            aligned = sum(g in ALIGNED for g in UNITS[u])
+            s_cols = W2_COLS_SCALAR - W2_COLS_ALIGNED * aligned // n
             s_cols += W2_COLS_SHIFT * (3 * u // len(UNITS) - 1)
             v_cols = D - s_cols
             w2_grouped[u] = w2_stage.tile(
@@ -227,9 +227,10 @@ def tile_vae_pb_k_kernel(tc, z, x, Wd1, bd1, Wd2, bd2, out):
 
         def regroup_hd(u):
             n = sum(g not in ALIGNED for g in UNITS[u])
-            regroup(
-                nc.vector.tensor_copy, hd_grouped[u][:, 0:n, :, :], hd_rows[u][:, 0:n, :, :]
-            )
+            if n > 0:
+                regroup(
+                    nc.vector.tensor_copy, hd_grouped[u][:, 0:n, :, :], hd_rows[u][:, 0:n, :, :]
+                )
 
         def quantise(grouped, n, width, name):
             codes = packed.tile(
@@ -284,19 +285,21 @@ def tile_vae_pb_k_kernel(tc, z, x, Wd1, bd1, Wd2, bd2, out):
                     (hidden_matmuls_aligned if g in ALIGNED else hidden_matmuls)(g)
             if 0 <= i + 1 < len(UNITS):
                 hidden_relu(i + 1)
+            if i > 0:
+                output_layer(i - 1)
             if i == 0:
                 spread_first_place()
             if i >= 0:
                 n = len(UNITS[i])
                 w2_packed[i] = quantise(w2_grouped[i], n, D, "w2")
                 hd_packed[i] = quantise(hd_grouped[i], n, B, "hd")
-                output_layer(i)
             if 0 < i + 2 < len(UNITS):
                 regroup_w2(i + 2)
                 if i + 2 + W2_RING < len(UNITS):
                     load_weights(i + 2 + W2_RING)
             if 0 <= i + 1 < len(UNITS):
                 regroup_hd(i + 1)
+        output_layer(len(UNITS) - 1)
 
         xv_sum = const.tile([P, B_TILES], F32)
         abs_sum = const.tile([P, B_TILES], F32)

@@ -19,18 +19,16 @@ B, D, L, H = 256, 512, 128, 16384
 PASSES = H // K_PASS
 B_TILES = B // P
 
-W1_LOAD_PASSES = 2
-W1_LOADS = PASSES // W1_LOAD_PASSES
 
 UNITS = [[0], [1]] + [[g, g + 1] for g in range(2, PASSES - 2, 2)] + [[PASSES - 2], [PASSES - 1]]
 UNIT_MAX = 2
-W2_RING = 9
+W2_RING = 8
 
 ALIGNED = [g for g in range(5, PASSES, 2) if g // 2 % 3 != 1]
 
-W2_COLS_SCALAR = 224
+W2_COLS_SCALAR = 216
 W2_COLS_ALIGNED = 80
-W2_COLS_SHIFT = 48
+W2_COLS_SHIFT = 40
 
 FLOPS = 2 * B * L * H + 2 * B * H * D
 
@@ -46,10 +44,10 @@ def tile_vae_pb_k_kernel(tc, z, x, Wd1, bd1, Wd2, bd2, out):
     nc = tc.nc
     with ExitStack() as ctx:
         const = ctx.enter_context(tc.tile_pool(name="const", bufs=1))
-        w1_pool = ctx.enter_context(tc.tile_pool(name="w1_pool", bufs=W1_LOADS))
+        w1_pool = ctx.enter_context(tc.tile_pool(name="w1_pool", bufs=len(UNITS)))
         w2_pool = ctx.enter_context(tc.tile_pool(name="w2_pool", bufs=W2_RING))
-        stage = ctx.enter_context(tc.tile_pool(name="stage", bufs=3))
-        w2_stage = ctx.enter_context(tc.tile_pool(name="w2_stage", bufs=4))
+        stage = ctx.enter_context(tc.tile_pool(name="stage", bufs=4))
+        w2_stage = ctx.enter_context(tc.tile_pool(name="w2_stage", bufs=5))
         packed = ctx.enter_context(tc.tile_pool(name="packed", bufs=3))
         tail = ctx.enter_context(tc.tile_pool(name="tail", bufs=2))
         psum_acc = ctx.enter_context(tc.psum_pool(name="psum_acc", bufs=1))
@@ -70,7 +68,7 @@ def tile_vae_pb_k_kernel(tc, z, x, Wd1, bd1, Wd2, bd2, out):
 
         load_bias(bd1_rows[0:PASSES, :])
 
-        w1_loaded = {}
+        w1_by_place = {}
         w2_rows = {}
 
         def load_weights(u):
@@ -82,16 +80,15 @@ def tile_vae_pb_k_kernel(tc, z, x, Wd1, bd1, Wd2, bd2, out):
                     "(s p t) n -> p s t n", p=P, t=PACK
                 ),
             )
-            for g in passes:
-                if g % W1_LOAD_PASSES == 0:
-                    w1_tile = w1_pool.tile([P, W1_LOAD_PASSES, K_PASS], BF16, name="w1_tile")
-                    nc.sync.dma_start(
-                        out=w1_tile[:],
-                        in_=Wd1[:, g * K_PASS : (g + W1_LOAD_PASSES) * K_PASS].rearrange(
-                            "l (s k) -> l s k", k=K_PASS
-                        ),
-                    )
-                    w1_loaded[g // W1_LOAD_PASSES] = w1_tile
+            w1_tile = w1_pool.tile([P, UNIT_MAX, K_PASS], BF16, name="w1_tile")
+            nc.sync.dma_start(
+                out=w1_tile[:, 0 : len(passes), :],
+                in_=Wd1[:, passes[0] * K_PASS : (passes[-1] + 1) * K_PASS].rearrange(
+                    "l (s k) -> l s k", k=K_PASS
+                ),
+            )
+            for s, g in enumerate(passes):
+                w1_by_place[g] = w1_tile[:, s, :].rearrange("l (p t) -> l t p", t=PACK)
 
         for u in range(W2_RING):
             load_weights(u)
@@ -141,16 +138,13 @@ def tile_vae_pb_k_kernel(tc, z, x, Wd1, bd1, Wd2, bd2, out):
         w2_packed = {}
 
         def hidden_matmuls(g):
-            w1_by_place = w1_loaded[g // W1_LOAD_PASSES][:, g % W1_LOAD_PASSES, :].rearrange(
-                "l (p t) -> l t p", t=PACK
-            )
             hid_banks[g] = []
             for half in range(2):
                 bank = psum.tile([P, 2, B], F32, name="hid", tag="work")
                 for j in range(2):
                     nc.tensor.matmul(
                         out=bank[:, j, :],
-                        lhsT=w1_by_place[:, 2 * half + j, :],
+                        lhsT=w1_by_place[g][:, 2 * half + j, :],
                         rhs=zT[:],
                         start=True,
                         stop=True,
@@ -160,9 +154,6 @@ def tile_vae_pb_k_kernel(tc, z, x, Wd1, bd1, Wd2, bd2, out):
         bias_by_place = bias_rows[:].rearrange("g (p t) -> g t p", t=PACK)
 
         def hidden_matmuls_aligned(g):
-            w1_by_place = w1_loaded[g // W1_LOAD_PASSES][:, g % W1_LOAD_PASSES, :].rearrange(
-                "l (p t) -> l t p", t=PACK
-            )
             hid_banks[g] = [
                 psum.tile([P, PACK, P], F32, name="hid", tag="work") for m in range(B_TILES)
             ]
@@ -170,7 +161,7 @@ def tile_vae_pb_k_kernel(tc, z, x, Wd1, bd1, Wd2, bd2, out):
                 for m in range(B_TILES):
                     nc.tensor.matmul(
                         out=hid_banks[g][m][:, t, :],
-                        lhsT=w1_by_place[:, t, :],
+                        lhsT=w1_by_place[g][:, t, :],
                         rhs=zT[:, m * P : (m + 1) * P],
                         start=True,
                         stop=(t == 0),
@@ -324,6 +315,9 @@ def tile_vae_pb_k_kernel(tc, z, x, Wd1, bd1, Wd2, bd2, out):
         for m in range(B_TILES):
             nc.scalar.activation(out=decay[m][:], in_=abs_v[m][:], func=ACT.Exp, scale=-1.0)
 
+        unused = tail.tile([P, 1], F32, name="unused")
+        nc.scalar.activation(out=unused[:], in_=ident_f32[:, 0:1], func=ACT.Ln, bias=1.0)
+
         def cross_term(m):
             xv = tail.tile([P, D], F32, name="xv")
             nc.vector.scalar_tensor_tensor(
@@ -338,22 +332,26 @@ def tile_vae_pb_k_kernel(tc, z, x, Wd1, bd1, Wd2, bd2, out):
 
         factors = const.tile([P, B_TILES, D // 2], F32)
 
+        upper = [tail.tile([P, D // 2], F32, name="upper") for m in range(B_TILES)]
+
+        def upper_factors(m):
+            nc.vector.tensor_scalar_add(upper[m][:], decay[m][:, D // 2 : D], 1.0)
+
         def multiply_factors(m):
-            upper = tail.tile([P, D // 2], F32, name="upper")
-            nc.vector.tensor_scalar_add(upper[:], decay[m][:, D // 2 : D], 1.0)
             nc.vector.scalar_tensor_tensor(
                 out=factors[:, m, :],
                 in0=decay[m][:, 0 : D // 2],
                 scalar=1.0,
-                in1=upper[:],
+                in1=upper[m][:],
                 op0=ALU.add,
                 op1=ALU.mult,
             )
 
         cross_term(0)
-        multiply_factors(0)
-        multiply_factors(1)
+        upper_factors(0)
         cross_term(1)
+        multiply_factors(0)
+        upper_factors(1)
         nc.vector.scalar_tensor_tensor(
             out=early_terms[:, 0:B_TILES],
             in0=abs_sum[:],
@@ -362,6 +360,7 @@ def tile_vae_pb_k_kernel(tc, z, x, Wd1, bd1, Wd2, bd2, out):
             op0=ALU.mult,
             op1=ALU.subtract,
         )
+        multiply_factors(1)
         for m in range(B_TILES):
             log_factors = tail.tile([P, D // 2], F32, name="log_factors")
             nc.scalar.activation(

@@ -26,9 +26,9 @@ W2_RING = 8
 
 ALIGNED = [g for g in range(5, PASSES, 2) if g // 2 % 3 != 1]
 
-W2_COLS_SCALAR = 216
+W2_COLS_SCALAR = 224
 W2_COLS_ALIGNED = 80
-W2_COLS_SHIFT = 40
+W2_COLS_SHIFT = 48
 
 FLOPS = 2 * B * L * H + 2 * B * H * D
 
@@ -63,10 +63,10 @@ def tile_vae_pb_k_kernel(tc, z, x, Wd1, bd1, Wd2, bd2, out):
         nc.vector.memset(bias_rows[2 * PASSES : P, :], 0.0)
         spare_rows = const.tile([P, K_PASS], BF16)
 
-        def load_bias(rows):
-            nc.scalar.dma_start(out=rows, in_=bd1.rearrange("(g k) -> g k", k=K_PASS))
+        def load_bias(queue, rows):
+            queue.dma_start(out=rows, in_=bd1.rearrange("(g k) -> g k", k=K_PASS))
 
-        load_bias(bd1_rows[0:PASSES, :])
+        load_bias(nc.scalar, bd1_rows[0:PASSES, :])
 
         w1_by_place = {}
         w2_rows = {}
@@ -92,8 +92,9 @@ def tile_vae_pb_k_kernel(tc, z, x, Wd1, bd1, Wd2, bd2, out):
 
         for u in range(W2_RING):
             load_weights(u)
-        load_bias(bias_rows[0:PASSES, :])
-        load_bias(spare_rows[PASSES : 2 * PASSES, :])
+            if u == 1:
+                load_bias(nc.sync, bias_rows[0:PASSES, :])
+                load_bias(nc.sync, spare_rows[PASSES : 2 * PASSES, :])
 
         x_sb = const.tile([P, B_TILES, D], BF16)
         nc.sync.dma_start(out=x_sb[:], in_=x.rearrange("(m p) d -> p m d", p=P))
@@ -278,8 +279,6 @@ def tile_vae_pb_k_kernel(tc, z, x, Wd1, bd1, Wd2, bd2, out):
                 hidden_relu(i + 1)
             if i > 0:
                 output_layer(i - 1)
-            if i == 0:
-                spread_first_place()
             if i >= 0:
                 n = len(UNITS[i])
                 w2_packed[i] = quantise(w2_grouped[i], n, D, "w2")
@@ -290,6 +289,8 @@ def tile_vae_pb_k_kernel(tc, z, x, Wd1, bd1, Wd2, bd2, out):
                     load_weights(i + 2 + W2_RING)
             if 0 <= i + 1 < len(UNITS):
                 regroup_hd(i + 1)
+            if i == 0:
+                spread_first_place()
         output_layer(len(UNITS) - 1)
 
         xv_sum = const.tile([P, B_TILES], F32)

@@ -48,7 +48,7 @@ def tile_vae_pb_k_kernel(tc, z, x, Wd1, bd1, Wd2, bd2, out):
         w2_pool = ctx.enter_context(tc.tile_pool(name="w2_pool", bufs=W2_RING))
         stage = ctx.enter_context(tc.tile_pool(name="stage", bufs=4))
         w2_stage = ctx.enter_context(tc.tile_pool(name="w2_stage", bufs=5))
-        packed = ctx.enter_context(tc.tile_pool(name="packed", bufs=3))
+        packed = ctx.enter_context(tc.tile_pool(name="packed", bufs=4))
         tail = ctx.enter_context(tc.tile_pool(name="tail", bufs=2))
         psum_acc = ctx.enter_context(tc.psum_pool(name="psum_acc", bufs=1))
         psum = ctx.enter_context(tc.psum_pool(name="psum", bufs=6))
@@ -67,6 +67,10 @@ def tile_vae_pb_k_kernel(tc, z, x, Wd1, bd1, Wd2, bd2, out):
             queue.dma_start(out=rows, in_=bd1.rearrange("(g k) -> g k", k=K_PASS))
 
         load_bias(nc.scalar, bd1_rows[0:PASSES, :])
+        one_column = const.tile([P, 1], F32)
+        nc.gpsimd.memset(one_column[:], 0.0)
+        unused = const.tile([P, 1], F32)
+        nc.scalar.activation(out=unused[:], in_=one_column[:], func=ACT.Sigmoid)
 
         w1_by_place = {}
         w2_rows = {}
@@ -103,8 +107,6 @@ def tile_vae_pb_k_kernel(tc, z, x, Wd1, bd1, Wd2, bd2, out):
 
         ident = const.tile([P, P], BF16)
         make_identity(nc, ident[:])
-        ident_f32 = const.tile([P, P], F32)
-        make_identity(nc, ident_f32[:])
         signs = const.tile([P, PASSES], BF16)
         nc.vector.tensor_tensor(
             out=signs[:], in0=ident[:, 0:PASSES], in1=ident[:, PASSES : 2 * PASSES], op=ALU.subtract
@@ -116,10 +118,10 @@ def tile_vae_pb_k_kernel(tc, z, x, Wd1, bd1, Wd2, bd2, out):
             .unsqueeze(2)
             .to_broadcast([P, PASSES // 2, P]),
         )
-        early_terms = const.tile([P, P], F32)
-        log_terms = const.tile([P, P], F32)
-        nc.gpsimd.memset(early_terms[:], 0.0)
-        nc.gpsimd.memset(log_terms[:], 0.0)
+        xv_terms = const.tile([P, B_TILES], F32)
+        log_terms = const.tile([P, B_TILES], F32)
+        sums = const.tile([P, 32], F32, align_bytes=64)
+        nc.gpsimd.memset(sums[:], 0.0)
 
         zT_ps = psum.tile([P, B], BF16, tag="work")
         for m in range(B_TILES):
@@ -279,88 +281,60 @@ def tile_vae_pb_k_kernel(tc, z, x, Wd1, bd1, Wd2, bd2, out):
                 hidden_relu(i + 1)
             if i > 0:
                 output_layer(i - 1)
+            if 0 < i + 1 < len(UNITS):
+                w2_packed[i + 1] = quantise(w2_grouped[i + 1], len(UNITS[i + 1]), D, "w2")
             if i >= 0:
-                n = len(UNITS[i])
-                w2_packed[i] = quantise(w2_grouped[i], n, D, "w2")
-                hd_packed[i] = quantise(hd_grouped[i], n, B, "hd")
+                hd_packed[i] = quantise(hd_grouped[i], len(UNITS[i]), B, "hd")
             if 0 < i + 2 < len(UNITS):
                 regroup_w2(i + 2)
                 if i + 2 + W2_RING < len(UNITS):
                     load_weights(i + 2 + W2_RING)
+            if i == -1:
+                w2_packed[0] = quantise(w2_grouped[0], len(UNITS[0]), D, "w2")
             if 0 <= i + 1 < len(UNITS):
                 regroup_hd(i + 1)
             if i == 0:
                 spread_first_place()
         output_layer(len(UNITS) - 1)
 
-        xv_sum = const.tile([P, B_TILES], F32)
-        abs_sum = const.tile([P, B_TILES], F32)
-        logits = []
-        for m in range(B_TILES):
-            logits.append(tail.tile([P, D], F32, name="logits"))
-            nc.vector.tensor_tensor(out=logits[m][:], in0=acc[m][:], in1=bd2_all[:], op=ALU.add)
-        abs_v = [tail.tile([P, D], F32, name="abs_v") for m in range(B_TILES)]
-        nc.scalar.activation(
-            out=abs_v[0][:], in_=logits[0][:], func=ACT.Abs, accum_out=abs_sum[:, 0:1]
-        )
-        nc.vector.scalar_tensor_tensor(
-            out=abs_v[1][:],
-            in0=logits[1][:],
-            scalar=-1.0,
-            in1=logits[1][:],
-            op0=ALU.mult,
-            op1=ALU.max,
-            accum_out=abs_sum[:, 1:2],
-        )
-        decay = [tail.tile([P, D], F32, name="decay") for m in range(B_TILES)]
-        for m in range(B_TILES):
-            nc.scalar.activation(out=decay[m][:], in_=abs_v[m][:], func=ACT.Exp, scale=-1.0)
+        logits = [tail.tile([P, D], F32, name="logits") for m in range(B_TILES)]
+        theta_bar = [tail.tile([P, D], F32, name="theta_bar") for m in range(B_TILES)]
+        halves = (slice(0, D // 2), slice(D // 2, D))
+        for m, cols in ((m, cols) for m in range(B_TILES) for cols in halves):
+            nc.vector.tensor_tensor(
+                out=logits[m][:, cols], in0=acc[m][:, cols], in1=bd2_all[:, cols], op=ALU.add
+            )
+            nc.scalar.activation(
+                out=theta_bar[m][:, cols], in_=logits[m][:, cols], func=ACT.Sigmoid, scale=-1.0
+            )
 
-        unused = tail.tile([P, 1], F32, name="unused")
-        nc.scalar.activation(out=unused[:], in_=ident_f32[:, 0:1], func=ACT.Ln, bias=1.0)
+        nc.scalar.activation(out=unused[:], in_=one_column[:], func=ACT.Ln, bias=1.0)
 
         def cross_term(m):
             xv = tail.tile([P, D], F32, name="xv")
             nc.vector.scalar_tensor_tensor(
                 out=xv[:],
                 in0=x_sb[:, m, :],
-                scalar=-0.5,
+                scalar=1.0,
                 in1=logits[m][:],
-                op0=ALU.add,
+                op0=ALU.mult,
                 op1=ALU.mult,
-                accum_out=xv_sum[:, m : m + 1],
+                accum_out=xv_terms[:, m : m + 1],
             )
 
         factors = const.tile([P, B_TILES, D // 2], F32)
 
-        upper = [tail.tile([P, D // 2], F32, name="upper") for m in range(B_TILES)]
-
-        def upper_factors(m):
-            nc.vector.tensor_scalar_add(upper[m][:], decay[m][:, D // 2 : D], 1.0)
-
         def multiply_factors(m):
-            nc.vector.scalar_tensor_tensor(
+            nc.vector.tensor_tensor(
                 out=factors[:, m, :],
-                in0=decay[m][:, 0 : D // 2],
-                scalar=1.0,
-                in1=upper[m][:],
-                op0=ALU.add,
-                op1=ALU.mult,
+                in0=theta_bar[m][:, 0 : D // 2],
+                in1=theta_bar[m][:, D // 2 : D],
+                op=ALU.mult,
             )
 
         cross_term(0)
-        upper_factors(0)
-        cross_term(1)
         multiply_factors(0)
-        upper_factors(1)
-        nc.vector.scalar_tensor_tensor(
-            out=early_terms[:, 0:B_TILES],
-            in0=abs_sum[:],
-            scalar=0.5,
-            in1=xv_sum[:],
-            op0=ALU.mult,
-            op1=ALU.subtract,
-        )
+        cross_term(1)
         multiply_factors(1)
         for m in range(B_TILES):
             log_factors = tail.tile([P, D // 2], F32, name="log_factors")
@@ -371,23 +345,13 @@ def tile_vae_pb_k_kernel(tc, z, x, Wd1, bd1, Wd2, bd2, out):
                 accum_out=log_terms[:, m : m + 1],
             )
 
-        sums_ps = psum.tile([P, P], F32, tag="work")
-        nc.tensor.matmul(
-            out=sums_ps[:],
-            lhsT=early_terms[:],
-            rhs=ident_f32[:],
-            is_transpose=True,
-            start=True,
-            stop=False,
+        nc.vector.tensor_tensor(
+            out=sums[:, 0:B_TILES], in0=xv_terms[:], in1=log_terms[:], op=ALU.add
         )
-        nc.tensor.matmul(
-            out=sums_ps[:],
-            lhsT=log_terms[:],
-            rhs=ident_f32[:],
-            is_transpose=True,
-            start=False,
-            stop=True,
-        )
-        result = const.tile([P, P], F32)
-        nc.vector.tensor_scalar_mul(result[:], sums_ps[:], -1.0)
-        nc.sync.dma_start(out=out.rearrange("(m p) -> m p", p=P), in_=result[0:B_TILES, :])
+        result = const.tile([P, 32], F32, align_bytes=64)
+        nc.vector.transpose(out=result[:], in_=sums[:])
+        for m, queue in enumerate((nc.sync, nc.scalar)):
+            queue.dma_start(
+                out=out[m * P : (m + 1) * P].rearrange("(q i) -> q i", i=32),
+                in_=result[m:P:32, :],
+            )

@@ -48,7 +48,7 @@ def tile_vae_pb_k_kernel(tc, z, x, Wd1, bd1, Wd2, bd2, out):
         w2_pool = ctx.enter_context(tc.tile_pool(name="w2_pool", bufs=W2_RING))
         stage = ctx.enter_context(tc.tile_pool(name="stage", bufs=4))
         w2_stage = ctx.enter_context(tc.tile_pool(name="w2_stage", bufs=5))
-        packed = ctx.enter_context(tc.tile_pool(name="packed", bufs=4))
+        packed = ctx.enter_context(tc.tile_pool(name="packed", bufs=3))
         tail = ctx.enter_context(tc.tile_pool(name="tail", bufs=2))
         psum_acc = ctx.enter_context(tc.psum_pool(name="psum_acc", bufs=1))
         psum = ctx.enter_context(tc.psum_pool(name="psum", bufs=6))
@@ -281,16 +281,14 @@ def tile_vae_pb_k_kernel(tc, z, x, Wd1, bd1, Wd2, bd2, out):
                 hidden_relu(i + 1)
             if i > 0:
                 output_layer(i - 1)
-            if 0 < i + 1 < len(UNITS):
-                w2_packed[i + 1] = quantise(w2_grouped[i + 1], len(UNITS[i + 1]), D, "w2")
             if i >= 0:
-                hd_packed[i] = quantise(hd_grouped[i], len(UNITS[i]), B, "hd")
+                n = len(UNITS[i])
+                w2_packed[i] = quantise(w2_grouped[i], n, D, "w2")
+                hd_packed[i] = quantise(hd_grouped[i], n, B, "hd")
             if 0 < i + 2 < len(UNITS):
                 regroup_w2(i + 2)
                 if i + 2 + W2_RING < len(UNITS):
                     load_weights(i + 2 + W2_RING)
-            if i == -1:
-                w2_packed[0] = quantise(w2_grouped[0], len(UNITS[0]), D, "w2")
             if 0 <= i + 1 < len(UNITS):
                 regroup_hd(i + 1)
             if i == 0:

@@ -107,6 +107,8 @@ def tile_vae_pb_k_kernel(tc, z, x, Wd1, bd1, Wd2, bd2, out):
 
         ident = const.tile([P, P], BF16)
         make_identity(nc, ident[:])
+        ident_f32 = const.tile([P, P], F32)
+        make_identity(nc, ident_f32[:])
         signs = const.tile([P, PASSES], BF16)
         nc.vector.tensor_tensor(
             out=signs[:], in0=ident[:, 0:PASSES], in1=ident[:, PASSES : 2 * PASSES], op=ALU.subtract
@@ -118,10 +120,10 @@ def tile_vae_pb_k_kernel(tc, z, x, Wd1, bd1, Wd2, bd2, out):
             .unsqueeze(2)
             .to_broadcast([P, PASSES // 2, P]),
         )
-        xv_terms = const.tile([P, B_TILES], F32)
-        log_terms = const.tile([P, B_TILES], F32)
-        sums = const.tile([P, 32], F32, align_bytes=64)
-        nc.gpsimd.memset(sums[:], 0.0)
+        xv_terms = const.tile([P, P], F32)
+        log_terms = const.tile([P, P], F32)
+        nc.gpsimd.memset(xv_terms[:], 0.0)
+        nc.gpsimd.memset(log_terms[:], 0.0)
 
         zT_ps = psum.tile([P, B], BF16, tag="work")
         for m in range(B_TILES):
@@ -343,13 +345,23 @@ def tile_vae_pb_k_kernel(tc, z, x, Wd1, bd1, Wd2, bd2, out):
                 accum_out=log_terms[:, m : m + 1],
             )
 
-        nc.vector.tensor_tensor(
-            out=sums[:, 0:B_TILES], in0=xv_terms[:], in1=log_terms[:], op=ALU.add
+        sums_ps = psum.tile([P, P], F32, tag="work")
+        nc.tensor.matmul(
+            out=sums_ps[:],
+            lhsT=xv_terms[:],
+            rhs=ident_f32[:],
+            is_transpose=True,
+            start=True,
+            stop=False,
         )
-        result = const.tile([P, 32], F32, align_bytes=64)
-        nc.vector.transpose(out=result[:], in_=sums[:])
-        for m, queue in enumerate((nc.sync, nc.scalar)):
-            queue.dma_start(
-                out=out[m * P : (m + 1) * P].rearrange("(q i) -> q i", i=32),
-                in_=result[m:P:32, :],
-            )
+        nc.tensor.matmul(
+            out=sums_ps[:],
+            lhsT=log_terms[:],
+            rhs=ident_f32[:],
+            is_transpose=True,
+            start=False,
+            stop=True,
+        )
+        result = const.tile([P, P], F32)
+        nc.vector.tensor_copy(out=result[:], in_=sums_ps[:])
+        nc.sync.dma_start(out=out.rearrange("(m p) -> m p", p=P), in_=result[0:B_TILES, :])

@@ -22,6 +22,7 @@ B_TILES = B // P
 
 UNITS = [[0], [1]] + [[g, g + 1] for g in range(2, PASSES - 2, 2)] + [[PASSES - 2], [PASSES - 1]]
 UNIT_MAX = 2
+EARLY_UNITS = 2
 W2_RING = 8
 
 ALIGNED = [g for g in range(5, PASSES, 2) if g // 2 % 3 != 1]
@@ -228,18 +229,20 @@ def tile_vae_pb_k_kernel(tc, z, x, Wd1, bd1, Wd2, bd2, out):
                     nc.vector.tensor_copy, hd_grouped[u][:, 0:n, :, :], hd_rows[u][:, 0:n, :, :]
                 )
 
-        def quantise(grouped, n, width, name):
+        def quantise(grouped, n, width, name, piece):
             codes = packed.tile(
                 [P, UNIT_MAX * width], U32, name=name + "_codes", align_bytes=64
             )
             scales = packed.tile(
                 [P, UNIT_MAX * width], U8, name=name + "_scales", align_bytes=64
             )
-            nc.vector.quantize_mx(
-                out=codes[:, 0 : n * width].bitcast(FP8X4),
-                scales=scales[:, 0 : n * width],
-                in_=grouped[:, 0:n, :, :].rearrange("p s c t -> p (s c t)"),
-            )
+            values = grouped[:].rearrange("p s c t -> p (s c t)")
+            for first in range(0, n * width, piece):
+                nc.vector.quantize_mx(
+                    out=codes[:, first : first + piece].bitcast(FP8X4),
+                    scales=scales[:, first : first + piece],
+                    in_=values[:, first * PACK : (first + piece) * PACK],
+                )
             return codes, scales
 
         acc = [psum_acc.tile([P, D], F32, name="acc%d" % m) for m in range(B_TILES)]
@@ -285,12 +288,17 @@ def tile_vae_pb_k_kernel(tc, z, x, Wd1, bd1, Wd2, bd2, out):
                 output_layer(i - 1)
             if i >= 0:
                 n = len(UNITS[i])
-                w2_packed[i] = quantise(w2_grouped[i], n, D, "w2")
-                hd_packed[i] = quantise(hd_grouped[i], n, B, "hd")
+                if i >= EARLY_UNITS:
+                    w2_packed[i] = quantise(w2_grouped[i], n, D, "w2", n * D)
+                last = i == len(UNITS) - 1
+                hd_packed[i] = quantise(hd_grouped[i], n, B, "hd", P if last else n * B)
             if 0 < i + 2 < len(UNITS):
                 regroup_w2(i + 2)
                 if i + 2 + W2_RING < len(UNITS):
                     load_weights(i + 2 + W2_RING)
+            if 0 <= i + 1 < EARLY_UNITS:
+                n = len(UNITS[i + 1])
+                w2_packed[i + 1] = quantise(w2_grouped[i + 1], n, D, "w2", n * D)
             if 0 <= i + 1 < len(UNITS):
                 regroup_hd(i + 1)
             if i == 0:

from contextlib import ExitStack

import concourse.mybir as mybir
from concourse.masks import make_identity

BF16 = mybir.dt.bfloat16
F32 = mybir.dt.float32
U8 = mybir.dt.uint8
U32 = mybir.dt.uint32
FP8X4 = mybir.dt.float8_e4m3fn_x4
ACT = mybir.ActivationFunctionType
ALU = mybir.AluOpType

P = 128
PACK = 4
K_PASS = P * PACK

B, D, L, H = 256, 512, 128, 16384
PASSES = H // K_PASS
B_TILES = B // P


UNITS = [[0], [1]] + [[g, g + 1] for g in range(2, PASSES - 2, 2)] + [[PASSES - 2], [PASSES - 1]]
UNIT_MAX = 2
EARLY_UNITS = 2
W2_RING = 8

ALIGNED = [g for g in range(5, PASSES, 2) if g // 2 % 3 != 1]

W2_COLS_SCALAR = 224
W2_COLS_ALIGNED = 80
W2_COLS_SHIFT = 48

FLOPS = 2 * B * L * H + 2 * B * H * D


def regroup(copy, grouped, rows):
    copy(
        out=grouped.rearrange("p s (c i) t -> p s c t i", i=8),
        in_=rows.rearrange("p s t (c i) -> p s c t i", i=8),
    )


def tile_vae_pb_k_kernel(tc, z, x, Wd1, bd1, Wd2, bd2, out):
    nc = tc.nc
    with ExitStack() as ctx:
        const = ctx.enter_context(tc.tile_pool(name="const", bufs=1))
        w1_pool = ctx.enter_context(tc.tile_pool(name="w1_pool", bufs=len(UNITS)))
        w2_pool = ctx.enter_context(tc.tile_pool(name="w2_pool", bufs=W2_RING))
        stage = ctx.enter_context(tc.tile_pool(name="stage", bufs=4))
        w2_stage = ctx.enter_context(tc.tile_pool(name="w2_stage", bufs=5))
        packed = ctx.enter_context(tc.tile_pool(name="packed", bufs=3))
        tail = ctx.enter_context(tc.tile_pool(name="tail", bufs=2))
        psum_acc = ctx.enter_context(tc.psum_pool(name="psum_acc", bufs=1))
        psum = ctx.enter_context(tc.psum_pool(name="psum", bufs=6))
        ctx.enter_context(tc.manual_schedule())

        z_sb = const.tile([P, B_TILES, L], BF16)
        nc.sync.dma_start(out=z_sb[:], in_=z.rearrange("(m p) l -> p m l", p=P))
        bd1_rows = const.tile([P, K_PASS], BF16)
        bias_rows = const.tile([P, K_PASS], BF16)
        for first, last in ((PASSES, 2 * PASSES), (2 * PASSES, P)):
            nc.vector.memset(bd1_rows[first:last, :], 0.0)
        nc.vector.memset(bias_rows[2 * PASSES : P, :], 0.0)
        spare_rows = const.tile([P, K_PASS], BF16)

        def load_bias(queue, rows):
            queue.dma_start(out=rows, in_=bd1.rearrange("(g k) -> g k", k=K_PASS))

        load_bias(nc.scalar, bd1_rows[0:PASSES, :])
        one_column = const.tile([P, 1], F32)
        nc.gpsimd.memset(one_column[:], 0.0)
        unused = const.tile([P, 1], F32)
        nc.scalar.activation(out=unused[:], in_=one_column[:], func=ACT.Sigmoid)

        w1_by_place = {}
        w2_rows = {}

        def load_weights(u):
            passes = UNITS[u]
            w2_rows[u] = w2_pool.tile([P, UNIT_MAX, PACK, D], BF16, name="w2_rows")
            nc.sync.dma_start(
                out=w2_rows[u][:, 0 : len(passes), :, :],
                in_=Wd2[passes[0] * K_PASS : (passes[-1] + 1) * K_PASS, :].rearrange(
                    "(s p t) n -> p s t n", p=P, t=PACK
                ),
            )
            w1_tile = w1_pool.tile([P, UNIT_MAX, K_PASS], BF16, name="w1_tile")
            nc.sync.dma_start(
                out=w1_tile[:, 0 : len(passes), :],
                in_=Wd1[:, passes[0] * K_PASS : (passes[-1] + 1) * K_PASS].rearrange(
                    "l (s k) -> l s k", k=K_PASS
                ),
            )
            for s, g in enumerate(passes):
                w1_by_place[g] = w1_tile[:, s, :].rearrange("l (p t) -> l t p", t=PACK)

        for u in range(W2_RING):
            load_weights(u)
            if u == 1:
                load_bias(nc.sync, bias_rows[0:PASSES, :])
                load_bias(nc.sync, spare_rows[PASSES : 2 * PASSES, :])

        x_sb = const.tile([P, B_TILES, D], BF16)
        nc.sync.dma_start(out=x_sb[:], in_=x.rearrange("(m p) d -> p m d", p=P))
        bd2_all = const.tile([P, D], BF16)
        nc.sync.dma_start(out=bd2_all[:], in_=bd2.partition_broadcast(P))

        ident = const.tile([P, P], BF16)
        make_identity(nc, ident[:])
        ident_f32 = const.tile([P, P], F32)
        make_identity(nc, ident_f32[:])
        signs = const.tile([P, PASSES], BF16)
        nc.vector.tensor_tensor(
            out=signs[:], in0=ident[:, 0:PASSES], in1=ident[:, PASSES : 2 * PASSES], op=ALU.subtract
        )
        pick = const.tile([P, PASSES // 2, P], BF16)
        nc.vector.tensor_copy(
            out=pick[:],
            in_=signs[:, 1:PASSES:2]
            .unsqueeze(2)
            .to_broadcast([P, PASSES // 2, P]),
        )
        xv_terms = const.tile([P, P], F32)
        log_terms = const.tile([P, P], F32)
        nc.gpsimd.memset(xv_terms[:], 0.0)
        nc.gpsimd.memset(log_terms[:], 0.0)

        zT_ps = psum.tile([P, B], BF16, tag="work")
        for m in range(B_TILES):
            nc.tensor.transpose(zT_ps[:, m * P : (m + 1) * P], z_sb[:, m, :], ident[:])
        zT = const.tile([P, B], BF16)

        bias_ps = psum.tile([P, PACK, P], BF16, tag="work")
        bd1_by_place = bd1_rows[:].rearrange("g (p t) -> g t p", t=PACK)
        for t in range(PACK):
            nc.tensor.transpose(bias_ps[:, t, :], bd1_by_place[:, t, :], ident[:])

        hid_banks = {}
        hd_rows = {}
        hd_grouped = {}
        w2_grouped = {}
        hd_packed = {}
        w2_packed = {}

        def hidden_matmuls(g):
            hid_banks[g] = []
            for half in range(2):
                bank = psum.tile([P, 2, B], F32, name="hid", tag="work")
                for j in range(2):
                    nc.tensor.matmul(
                        out=bank[:, j, :],
                        lhsT=w1_by_place[g][:, 2 * half + j, :],
                        rhs=zT[:],
                        start=True,
                        stop=True,
                    )
                hid_banks[g].append(bank)

        bias_by_place = bias_rows[:].rearrange("g (p t) -> g t p", t=PACK)

        def hidden_matmuls_aligned(g):
            hid_banks[g] = [
                psum.tile([P, PACK, P], F32, name="hid", tag="work") for m in range(B_TILES)
            ]
            for t in range(PACK):
                for m in range(B_TILES):
                    nc.tensor.matmul(
                        out=hid_banks[g][m][:, t, :],
                        lhsT=w1_by_place[g][:, t, :],
                        rhs=zT[:, m * P : (m + 1) * P],
                        start=True,
                        stop=(t == 0),
                    )
                    if t > 0:
                        nc.tensor.matmul(
                            out=hid_banks[g][m][:, t, :],
                            lhsT=bias_by_place[:, t, :],
                            rhs=pick[:, g // 2, :],
                            start=False,
                            stop=True,
                        )

        def hidden_relu(u):
            hd_grouped[u] = stage.tile(
                [P, UNIT_MAX, B, PACK], BF16, name="hd_grouped", align_bytes=64
            )
            if UNITS[u][0] not in ALIGNED:
                hd_rows[u] = stage.tile([P, UNIT_MAX, PACK, B], BF16, name="hd_rows")
            for s, g in enumerate(UNITS[u]):
                if g in ALIGNED:
                    for m in range(B_TILES):
                        nc.scalar.activation(
                            out=hd_grouped[u][:, s, m * P : (m + 1) * P, :],
                            in_=hid_banks[g][m][:].rearrange("p t b -> p b t"),
                            func=ACT.Relu,
                            bias=bias1[:, 0, g : g + 1],
                            scale=1.0,
                        )
                else:
                    for t in range(PACK):
                        nc.scalar.activation(
                            out=hd_rows[u][:, s, t, :],
                            in_=hid_banks[g][t // 2][:, t % 2, :],
                            func=ACT.Relu,
                            bias=bias1[:, t, g : g + 1],
                            scale=1.0,
                        )

        def regroup_w2(u):
            n = len(UNITS[u])
            aligned = sum(g in ALIGNED for g in UNITS[u])
            s_cols = W2_COLS_SCALAR - W2_COLS_ALIGNED * aligned // n
            s_cols += W2_COLS_SHIFT * (3 * u // len(UNITS) - 1)
            v_cols = D - s_cols
            w2_grouped[u] = w2_stage.tile(
                [P, UNIT_MAX, D, PACK], BF16, name="w2_grouped", align_bytes=64
            )
            for copy, cols in (
                (nc.scalar.copy, slice(v_cols, D)),
                (nc.vector.tensor_copy, slice(0, v_cols)),
            ):
                regroup(copy, w2_grouped[u][:, 0:n, cols, :], w2_rows[u][:, 0:n, :, cols])

        def regroup_hd(u):
            n = sum(g not in ALIGNED for g in UNITS[u])
            if n > 0:
                regroup(
                    nc.vector.tensor_copy, hd_grouped[u][:, 0:n, :, :], hd_rows[u][:, 0:n, :, :]
                )

        def quantise(grouped, n, width, name, piece):
            codes = packed.tile(
                [P, UNIT_MAX * width], U32, name=name + "_codes", align_bytes=64
            )
            scales = packed.tile(
                [P, UNIT_MAX * width], U8, name=name + "_scales", align_bytes=64
            )
            values = grouped[:].rearrange("p s c t -> p (s c t)")
            for first in range(0, n * width, piece):
                nc.vector.quantize_mx(
                    out=codes[:, first : first + piece].bitcast(FP8X4),
                    scales=scales[:, first : first + piece],
                    in_=values[:, first * PACK : (first + piece) * PACK],
                )
            return codes, scales

        acc = [psum_acc.tile([P, D], F32, name="acc%d" % m) for m in range(B_TILES)]

        def output_layer(u):
            hd_codes, hd_scales = hd_packed[u]
            w2_codes, w2_scales = w2_packed[u]
            for s, g in enumerate(UNITS[u]):
                for m in range(B_TILES):
                    rows_m = slice(s * B + m * P, s * B + (m + 1) * P)
                    cols = slice(s * D, (s + 1) * D)
                    nc.tensor.matmul_mx(
                        out=acc[m][:],
                        lhsT=hd_codes[:, rows_m].bitcast(FP8X4),
                        lhsT_scale=hd_scales[:, rows_m],
                        rhs=w2_codes[:, cols].bitcast(FP8X4),
                        rhs_scale=w2_scales[:, cols],
                        start=(g == 0),
                        stop=(g == PASSES - 1),
                    )

        def spread_first_place():
            nc.vector.tensor_copy(
                out=bias_rows[PASSES : 2 * PASSES, :].rearrange("g (p t) -> g p t", t=PACK),
                in_=spare_rows[PASSES : 2 * PASSES, :]
                .rearrange("g (p t) -> g p t", t=PACK)[:, :, 0:1]
                .to_broadcast([PASSES, P, PACK]),
            )

        nc.vector.tensor_copy(out=zT[:], in_=zT_ps[:])
        regroup_w2(0)
        load_weights(W2_RING)
        bias1 = const.tile([P, PACK, PASSES], F32)
        nc.vector.tensor_copy(out=bias1[:], in_=bias_ps[:, :, 0:PASSES])

        for i in range(-2, len(UNITS)):
            if i + 2 < len(UNITS):
                for g in UNITS[i + 2]:
                    (hidden_matmuls_aligned if g in ALIGNED else hidden_matmuls)(g)
            if 0 <= i + 1 < len(UNITS):
                hidden_relu(i + 1)
            if i > 0:
                output_layer(i - 1)
            if i >= 0:
                n = len(UNITS[i])
                if i >= EARLY_UNITS:
                    w2_packed[i] = quantise(w2_grouped[i], n, D, "w2", n * D)
                last = i == len(UNITS) - 1
                hd_packed[i] = quantise(hd_grouped[i], n, B, "hd", P if last else n * B)
            if 0 < i + 2 < len(UNITS):
                regroup_w2(i + 2)
                if i + 2 + W2_RING < len(UNITS):
                    load_weights(i + 2 + W2_RING)
            if 0 <= i + 1 < EARLY_UNITS:
                n = len(UNITS[i + 1])
                w2_packed[i + 1] = quantise(w2_grouped[i + 1], n, D, "w2", n * D)
            if 0 <= i + 1 < len(UNITS):
                regroup_hd(i + 1)
            if i == 0:
                spread_first_place()
        output_layer(len(UNITS) - 1)

        logits = [tail.tile([P, D], F32, name="logits") for m in range(B_TILES)]
        theta_bar = [tail.tile([P, D], F32, name="theta_bar") for m in range(B_TILES)]
        halves = (slice(0, D // 2), slice(D // 2, D))
        for m, cols in ((m, cols) for m in range(B_TILES) for cols in halves):
            nc.vector.tensor_tensor(
                out=logits[m][:, cols], in0=acc[m][:, cols], in1=bd2_all[:, cols], op=ALU.add
            )
            nc.scalar.activation(
                out=theta_bar[m][:, cols], in_=logits[m][:, cols], func=ACT.Sigmoid, scale=-1.0
            )

        nc.scalar.activation(out=unused[:], in_=one_column[:], func=ACT.Ln, bias=1.0)

        def cross_term(m):
            xv = tail.tile([P, D], F32, name="xv")
            nc.vector.scalar_tensor_tensor(
                out=xv[:],
                in0=x_sb[:, m, :],
                scalar=1.0,
                in1=logits[m][:],
                op0=ALU.mult,
                op1=ALU.mult,
                accum_out=xv_terms[:, m : m + 1],
            )

        factors = const.tile([P, B_TILES, D // 2], F32)

        def multiply_factors(m):
            nc.vector.tensor_tensor(
                out=factors[:, m, :],
                in0=theta_bar[m][:, 0 : D // 2],
                in1=theta_bar[m][:, D // 2 : D],
                op=ALU.mult,
            )

        cross_term(0)
        multiply_factors(0)
        cross_term(1)
        multiply_factors(1)
        for m in range(B_TILES):
            log_factors = tail.tile([P, D // 2], F32, name="log_factors")
            nc.scalar.activation(
                out=log_factors[:],
                in_=factors[:, m, :],
                func=ACT.Ln,
                accum_out=log_terms[:, m : m + 1],
            )

        sums_ps = psum.tile([P, P], F32, tag="work")
        nc.tensor.matmul(
            out=sums_ps[:],
            lhsT=xv_terms[:],
            rhs=ident_f32[:],
            is_transpose=True,
            start=True,
            stop=False,
        )
        nc.tensor.matmul(
            out=sums_ps[:],
            lhsT=log_terms[:],
            rhs=ident_f32[:],
            is_transpose=True,
            start=False,
            stop=True,
        )
        result = const.tile([P, P], F32)
        nc.vector.tensor_copy(out=result[:], in_=sums_ps[:])
        nc.sync.dma_start(out=out.rearrange("(m p) -> m p", p=P), in_=result[0:B_TILES, :])
